import numpy as np
import ml_dtypes


def mxq(x, axis, fmt="e4m3"):
    dtype, down = {"e4m3": (ml_dtypes.float8_e4m3fn, 7), "e5m2": (ml_dtypes.float8_e5m2, 14)}[fmt]
    v = np.moveaxis(np.asarray(x, np.float32).astype(ml_dtypes.bfloat16).astype(np.float64), axis, -1)
    blocks = v.reshape(v.shape[:-1] + (-1, 32))
    amax = np.abs(blocks).max(-1, keepdims=True)
    byte = np.maximum(np.where(amax > 0, np.frexp(amax)[1] - 1 + 127, 0) - down, 1)
    scale = np.exp2(byte - 127.0)
    codes = (blocks / scale).astype(np.float32).astype(dtype).astype(np.float64)
    return np.moveaxis((codes * scale).reshape(v.shape), -1, axis)


WIDE = False


def mx_kscale(k):
    if not WIDE:
        return np.ones(k)
    levels = np.array([10, -10, 5, -5, 0])
    a = np.random.permutation(np.resize(levels, k // 512 * 4)).reshape(k // 512, 4)
    idx = np.arange(k)
    return np.exp2(a[idx // 512, idx % 128 // 32])


BF16 = ml_dtypes.bfloat16


def bf(x):
    return np.asarray(x, np.float32).astype(BF16)


def f64(x):
    return np.asarray(x).astype(np.float64)


B, S, D, H, C = 1, 1024, 1024, 1024, 512
F = 2 * D
LN_EPS = 1e-5


def erf(u):
    a = np.clip(u, -6.0, 6.0)
    w = 2.0 * a * a
    term = a.copy()
    tot = a.copy()
    for n in range(1, 100):
        term = term * w / (2 * n + 1)
        tot = tot + term
    return 2.0 / np.sqrt(np.pi) * np.exp(-a * a) * tot


def gelu_erf(z):
    return 0.5 * z * (1.0 + erf(z / np.sqrt(2.0)))


def setup_inputs():
    s = mx_kscale(H)
    return {"h_ret": bf(np.random.standard_normal((B, S, H)) * 3.0 * s),
            "x": bf(np.random.standard_normal((B, S, D))),
            "W1": bf(np.random.standard_normal((F, H)) * 0.3 / np.sqrt(H) / s),
            "b1": bf(np.random.standard_normal(F) * 0.2),
            "W2": bf(np.random.standard_normal((D, F)) * 1.5 / np.sqrt(F)),
            "b2": bf(np.random.standard_normal(D) * 0.2),
            "ln_g": bf(1.0 + 0.1 * np.random.standard_normal(D)),
            "ln_b": bf(0.1 * np.random.standard_normal(D))}


def reference(h_ret, x, W1, b1, W2, b2, ln_g, ln_b):
    z = (mxq(f64(h_ret), 2, "e4m3") @ mxq(f64(W1), 1, "e4m3").T) + f64(b1)
    g = gelu_erf(z)
    o = (mxq(g, 2, "e4m3") @ mxq(f64(W2), 1, "e4m3").T) + f64(b2)
    y = f64(x) + o
    mu = y.mean(-1, keepdims=True)
    var = np.square(y - mu).mean(-1, keepdims=True)
    return (y - mu) / np.sqrt(var + LN_EPS) * f64(ln_g) + f64(ln_b)

@@ -1,0 +1,230 @@
+from contextlib import ExitStack
+
+import concourse.mybir as mybir
+from concourse.masks import make_identity
+
+F32 = mybir.dt.float32
+BF16 = mybir.dt.bfloat16
+U32 = mybir.dt.uint32
+U8 = mybir.dt.uint8
+FP8X4 = mybir.dt.float8_e4m3fn_x4
+ALU = mybir.AluOpType
+ACT = mybir.ActivationFunctionType
+
+P = 128
+PACK = 4
+K_PASS = P * PACK
+GROUP = 512
+TILES = GROUP // P
+
+S, H, F, D = 1024, 1024, 2048, 1024
+LN_EPS = 1e-5
+FLOPS = 2 * S * H * F + 2 * S * F * D
+
+
+def tile_simplifiedretnet_pb_kernel(tc, h_ret, x, W1, b1, W2, b2, ln_g, ln_b, out):
+    nc = tc.nc
+    with ExitStack() as ctx:
+        keep = ctx.enter_context(tc.tile_pool(name="keep", bufs=1))
+        raw = ctx.enter_context(tc.tile_pool(name="raw", bufs=4))
+        stage = ctx.enter_context(tc.tile_pool(name="stage", bufs=2))
+        stats = ctx.enter_context(tc.tile_pool(name="stats", bufs=4))
+        psum = ctx.enter_context(tc.psum_pool(name="psum", bufs=8))
+
+        def load_tokens(dram_rows):
+            rows = raw.tile([P, TILES * H], BF16, tag="h_then_x", bufs=2)
+            nc.sync.dma_start(out=rows[:], in_=dram_rows)
+            return rows
+
+        b1_bf = keep.tile([P, F // P], BF16)
+        nc.scalar.dma_start(
+            out=b1_bf[:].rearrange("m (a e) -> m a e", e=2),
+            in_=b1.rearrange("(a m e) -> m a e", m=P, e=2),
+        )
+
+        tokens = "(n m r) k -> n m (r k)"
+        h_groups = h_ret.flatten_outer_dims().rearrange(tokens, m=P, r=TILES)
+        x_groups = x.flatten_outer_dims().rearrange(tokens, m=P, r=TILES)
+        out_groups = out.flatten_outer_dims().rearrange("(n m r) d -> n m r d", m=P, r=TILES)
+        h_raw = [load_tokens(h_groups[n]) for n in range(S // GROUP)]
+
+        w1_groups = W1.rearrange("(c u m e) k -> c m u (e k)", u=2, m=P, e=2)
+        w1_raw = []
+        for c in range(F // GROUP):
+            rows = raw.tile([P, TILES * H], BF16, tag="w1_then_xb")
+            nc.sync.dma_start(out=rows[:].rearrange("m (u k) -> m u k", u=2), in_=w1_groups[c])
+            w1_raw.append(rows)
+
+        ident = keep.tile([P, P], F32)
+        make_identity(nc, ident[:])
+        minus_half = keep.tile([P, 1], F32)
+        nc.vector.memset(minus_half[:], -0.5)
+        b1_f32 = keep.tile([P, F // P], F32)
+        nc.vector.tensor_copy(out=b1_f32[:], in_=b1_bf[:])
+
+        h_codes = keep.tile([P, H // K_PASS, S], U32, align_bytes=64)
+        h_scales = keep.tile([P, H // K_PASS, S], U8, align_bytes=64)
+        w1_codes = keep.tile([P, H // K_PASS, F], U32, align_bytes=64)
+        w1_scales = keep.tile([P, H // K_PASS, F], U8, align_bytes=64)
+        w2_codes = keep.tile([P, F // K_PASS, D], U32, align_bytes=64)
+        w2_scales = keep.tile([P, F // K_PASS, D], U8, align_bytes=64)
+        g_codes = keep.tile([P, F // K_PASS, S], U32, align_bytes=64)
+        g_scales = keep.tile([P, F // K_PASS, S], U8, align_bytes=64)
+
+        def transpose_and_quantise(row_tiles, c, codes, scales):
+            grouped = stage.tile([P, GROUP * PACK], BF16, align_bytes=64, tag="grouped", bufs=3)
+            grouped_words = grouped[:].bitcast(F32).rearrange("p (r u) -> p r u", u=2)
+            for half in range(2):
+                bank = psum.tile([P, 2, 2 * P], F32, tag="bank")
+                for r in range(2):
+                    for u in range(2):
+                        first = (2 * c + u) * P
+                        nc.tensor.transpose(
+                            bank[:, u, r * P : (r + 1) * P],
+                            row_tiles[2 * half + r][:, first : first + P],
+                            ident[:],
+                        )
+                nc.scalar.copy(
+                    out=grouped_words[:, half * 2 * P : (half + 1) * 2 * P, :],
+                    in_=bank[:].rearrange("p u r -> p r u"),
+                )
+            nc.vector.quantize_mx(out=codes.bitcast(FP8X4), scales=scales, in_=grouped[:])
+
+        def word_tiles(rows, n):
+            words = rows[:].bitcast(F32).rearrange("m (r w) -> m r w", r=n)
+            return [words[:, r, :] for r in range(n)]
+
+        def first_product(c2, n):
+            tok = slice(n * GROUP, (n + 1) * GROUP)
+            g_plain = stage.tile([P, PACK, GROUP], BF16, tag="g_plain")
+            for t in range(PACK):
+                rows = slice(c2 * GROUP + t * P, c2 * GROUP + (t + 1) * P)
+                acc = psum.tile([P, GROUP], F32, tag="bank")
+                for c in range(H // K_PASS):
+                    nc.tensor.matmul_mx(
+                        out=acc[:],
+                        lhsT=w1_codes[:, c, rows].bitcast(FP8X4),
+                        lhsT_scale=w1_scales[:, c, rows],
+                        rhs=h_codes[:, c, tok].bitcast(FP8X4),
+                        rhs_scale=h_scales[:, c, tok],
+                        start=(c == 0),
+                        stop=(c == H // K_PASS - 1),
+                    )
+                j = c2 * PACK + t
+                nc.scalar.activation(
+                    out=g_plain[:, t, :], in_=acc[:], func=ACT.Gelu, bias=b1_f32[:, j : j + 1], scale=1.0
+                )
+            grouped = stage.tile([P, GROUP * PACK], BF16, align_bytes=64, tag="grouped", bufs=3)
+            nc.vector.tensor_copy(
+                out=grouped[:].rearrange("p (a i t) -> p a t i", i=4, t=PACK),
+                in_=g_plain[:].rearrange("p t (a i) -> p a t i", i=4),
+            )
+            nc.vector.quantize_mx(
+                out=g_codes[:, c2, tok].bitcast(FP8X4), scales=g_scales[:, c2, tok], in_=grouped[:]
+            )
+
+        xb_tiles = []
+
+        def add_bias_to_residual(n):
+            for pair in range(TILES // 2):
+                xb = raw.tile([P, 2, D], F32, tag="w1_then_xb")
+                for i in range(2):
+                    r = 2 * pair + i
+                    nc.vector.tensor_tensor(
+                        out=xb[:, i, :], in0=x_raw[n][:, r * D : (r + 1) * D], in1=b2_all[:], op=ALU.add
+                    )
+                    xb_tiles.append(xb[:, i, :])
+
+        def second_product_and_norm(n, r):
+            tok = slice(n * GROUP + r * P, n * GROUP + (r + 1) * P)
+            y = stage.tile([P, D], F32, tag="y")
+            sums = stats.tile([P, 2], F32, tag="sums")
+            for half in range(D // GROUP):
+                cols = slice(half * GROUP, (half + 1) * GROUP)
+                acc = psum.tile([P, GROUP], F32, tag="bank")
+                for c in range(F // K_PASS):
+                    nc.tensor.matmul_mx(
+                        out=acc[:],
+                        lhsT=g_codes[:, c, tok].bitcast(FP8X4),
+                        lhsT_scale=g_scales[:, c, tok],
+                        rhs=w2_codes[:, c, cols].bitcast(FP8X4),
+                        rhs_scale=w2_scales[:, c, cols],
+                        start=(c == 0),
+                        stop=(c == F // K_PASS - 1),
+                    )
+                nc.vector.scalar_tensor_tensor(
+                    out=y[:, cols],
+                    in0=acc[:],
+                    scalar=1.0,
+                    in1=xb_tiles[n * TILES + r][:, cols],
+                    op0=ALU.mult,
+                    op1=ALU.add,
+                    accum_out=sums[:, half : half + 1],
+                )
+            neg_mean = stats.tile([P, 2], F32, tag="neg_mean")
+            nc.vector.tensor_scalar(
+                out=neg_mean[:, 0:1], in0=sums[:, 0:1], scalar1=sums[:, 1:2], scalar2=-1.0 / D,
+                op0=ALU.add, op1=ALU.mult,
+            )
+            nc.vector.tensor_scalar(
+                out=neg_mean[:, 1:2], in0=sums[:, 0:1], scalar1=sums[:, 1:2], scalar2=-1.0 / (32.0 * D),
+                op0=ALU.add, op1=ALU.mult,
+            )
+            squares = stage.tile([P, D], BF16, tag="squares", bufs=1)
+            var = stats.tile([P, 1], F32, tag="var")
+            nc.scalar.activation(
+                out=squares[:], in_=y[:], func=ACT.Square, bias=neg_mean[:, 1:2], scale=1.0 / 32.0,
+                accum_out=var[:],
+            )
+            rstd = stats.tile([P, 2], F32, tag="rstd")
+            nc.gpsimd.tensor_scalar(
+                out=rstd[:, 0:1], in0=var[:], scalar1=1.0, scalar2=LN_EPS, op0=ALU.mult, op1=ALU.add
+            )
+            nc.gpsimd.tensor_tensor(out=rstd[:, 1:2], in0=rstd[:, 0:1], in1=minus_half[:], op=ALU.pow)
+            normed = stage.tile([P, D], F32, tag="normed", bufs=3)
+            nc.vector.scalar_tensor_tensor(
+                out=normed[:], in0=y[:], scalar=neg_mean[:, 0:1], in1=gain_all[:], op0=ALU.add, op1=ALU.mult
+            )
+            nc.vector.scalar_tensor_tensor(
+                out=normed[:], in0=normed[:], scalar=rstd[:, 1:2], in1=shift_all[:], op0=ALU.mult, op1=ALU.add
+            )
+            nc.sync.dma_start(out=out_groups[n][:, r, :], in_=normed[:])
+
+        for n in range(S // GROUP):
+            tok = slice(n * GROUP, (n + 1) * GROUP)
+            for c in range(H // K_PASS):
+                transpose_and_quantise(word_tiles(h_raw[n], TILES), c, h_codes[:, c, tok], h_scales[:, c, tok])
+
+        b2_all = keep.tile([P, D], BF16)
+        nc.sync.dma_start(out=b2_all[:], in_=b2.partition_broadcast(P))
+        x_raw = [load_tokens(x_groups[0])]
+        w2_pairs = W2.rearrange("(n r m) k -> n m r k", r=2, m=P)
+        w2_raw = []
+        for n in range(D // (2 * P)):
+            rows = raw.tile([P, 2 * F], BF16, tag="w2")
+            nc.sync.dma_start(out=rows[:].rearrange("m (r k) -> m r k", r=2), in_=w2_pairs[n])
+            w2_raw.append(rows)
+        x_raw.append(load_tokens(x_groups[1]))
+        gain_all = keep.tile([P, D], BF16)
+        nc.sync.dma_start(out=gain_all[:], in_=ln_g.partition_broadcast(P))
+        shift_all = keep.tile([P, D], BF16)
+        nc.sync.dma_start(out=shift_all[:], in_=ln_b.partition_broadcast(P))
+
+        for c2 in range(F // GROUP):
+            rows = slice(c2 * GROUP, (c2 + 1) * GROUP)
+            for c in range(H // K_PASS):
+                transpose_and_quantise(word_tiles(w1_raw[c2], TILES), c, w1_codes[:, c, rows], w1_scales[:, c, rows])
+            first_product(c2, 0)
+        add_bias_to_residual(0)
+        for half in range(D // GROUP):
+            cols = slice(half * GROUP, (half + 1) * GROUP)
+            row_tiles = word_tiles(w2_raw[2 * half], 2) + word_tiles(w2_raw[2 * half + 1], 2)
+            for c in range(F // K_PASS):
+                transpose_and_quantise(row_tiles, c, w2_codes[:, c, cols], w2_scales[:, c, cols])
+        for r in range(TILES):
+            second_product_and_norm(0, r)
+        for c2 in range(F // GROUP):
+            first_product(c2, 1)
+        add_bias_to_residual(1)
+        for r in range(TILES):
+            second_product_and_norm(1, r)

@@ -30,15 +30,15 @@ def tile_simplifiedretnet_pb_kernel(tc, h_ret, x, W1, b1, W2, b2, ln_g, ln_b, ou
         stage = ctx.enter_context(tc.tile_pool(name="stage", bufs=2))
         stats = ctx.enter_context(tc.tile_pool(name="stats", bufs=4))
         psum = ctx.enter_context(tc.psum_pool(name="psum", bufs=8))
+        ctx.enter_context(tc.manual_schedule())
 
-        def load_tokens(dram_rows):
-            rows = raw.tile([P, TILES * H], BF16, tag="h_then_x", bufs=2)
-            nc.sync.dma_start(out=rows[:], in_=dram_rows)
-            return rows
-
-        b1_bf = keep.tile([P, F // P], BF16)
+        row0 = keep.tile([P, 3 * D], BF16)
+        nc.vector.memset(row0[:].bitcast(F32), 0.0)
+        for i, vector in enumerate((b2, ln_g, ln_b)):
+            nc.scalar.dma_start(out=row0[0:1, i * D : (i + 1) * D], in_=vector.unsqueeze(0))
+        b1_cols = keep.tile([P, F // P], BF16)
         nc.scalar.dma_start(
-            out=b1_bf[:].rearrange("m (a e) -> m a e", e=2),
+            out=b1_cols[:].rearrange("m (a e) -> m a e", e=2),
             in_=b1.rearrange("(a m e) -> m a e", m=P, e=2),
         )
 
@@ -46,21 +46,53 @@ def tile_simplifiedretnet_pb_kernel(tc, h_ret, x, W1, b1, W2, b2, ln_g, ln_b, ou
         h_groups = h_ret.flatten_outer_dims().rearrange(tokens, m=P, r=TILES)
         x_groups = x.flatten_outer_dims().rearrange(tokens, m=P, r=TILES)
         out_groups = out.flatten_outer_dims().rearrange("(n m r) d -> n m r d", m=P, r=TILES)
-        h_raw = [load_tokens(h_groups[n]) for n in range(S // GROUP)]
-
         w1_groups = W1.rearrange("(c u m e) k -> c m u (e k)", u=2, m=P, e=2)
-        w1_raw = []
-        for c in range(F // GROUP):
+        w2_pairs = W2.rearrange("(n r m) k -> n m r k", r=2, m=P)
+
+        def load_tokens(dram_rows, tag):
+            rows = raw.tile([P, TILES * H], BF16, tag=tag, bufs=2)
+            nc.sync.dma_start(out=rows[:], in_=dram_rows)
+            return rows
+
+        def load_w1(c):
             rows = raw.tile([P, TILES * H], BF16, tag="w1_then_xb")
             nc.sync.dma_start(out=rows[:].rearrange("m (u k) -> m u k", u=2), in_=w1_groups[c])
-            w1_raw.append(rows)
+            return rows
+
+        def load_w2(n):
+            rows = raw.tile([P, 2 * F], BF16, tag="w2")
+            nc.sync.dma_start(out=rows[:].rearrange("m (r k) -> m r k", r=2), in_=w2_pairs[n])
+            return rows
+
+        h_raw = [load_tokens(h_groups[0], "h")]
+        w1_raw = [load_w1(0), load_w1(1)]
+        x_raw = [load_tokens(x_groups[0], "x")]
+        w1_raw.extend([load_w1(2), load_w1(3)])
+        x_raw.append(load_tokens(x_groups[1], "x"))
+        w2_raw = [load_w2(n) for n in range(D // (2 * P))]
+        h_raw.append(load_tokens(h_groups[1], "h"))
 
         ident = keep.tile([P, P], F32)
         make_identity(nc, ident[:])
         minus_half = keep.tile([P, 1], F32)
         nc.vector.memset(minus_half[:], -0.5)
-        b1_f32 = keep.tile([P, F // P], F32)
-        nc.vector.tensor_copy(out=b1_f32[:], in_=b1_bf[:])
+        ones = keep.tile([P, P], BF16)
+        nc.vector.memset(ones[:], 1.0)
+        warm = keep.tile([P, 1], F32)
+        nc.scalar.activation(out=warm[:], in_=minus_half[:], func=ACT.Gelu)
+
+        def group(n):
+            return slice(n * GROUP, (n + 1) * GROUP)
+
+        repeated = keep.tile([P, 3 * D], BF16)
+        for j in range(3 * D // GROUP):
+            acc = psum.tile([P, GROUP], F32, tag="bank")
+            nc.tensor.matmul(out=acc[:], lhsT=ones[:], rhs=row0[:, group(j)], start=True, stop=True)
+            if j % 2 == 0:
+                nc.vector.tensor_copy(out=repeated[:, group(j)], in_=acc[:])
+            else:
+                nc.scalar.copy(out=repeated[:, group(j)], in_=acc[:])
+        b2_all, gain_all, shift_all = [repeated[:, i * D : (i + 1) * D] for i in range(3)]
 
         h_codes = keep.tile([P, H // K_PASS, S], U32, align_bytes=64)
         h_scales = keep.tile([P, H // K_PASS, S], U8, align_bytes=64)
@@ -71,9 +103,27 @@ def tile_simplifiedretnet_pb_kernel(tc, h_ret, x, W1, b1, W2, b2, ln_g, ln_b, ou
         g_codes = keep.tile([P, F // K_PASS, S], U32, align_bytes=64)
         g_scales = keep.tile([P, F // K_PASS, S], U8, align_bytes=64)
 
-        def transpose_and_quantise(row_tiles, c, codes, scales):
-            grouped = stage.tile([P, GROUP * PACK], BF16, align_bytes=64, tag="grouped", bufs=3)
-            grouped_words = grouped[:].bitcast(F32).rearrange("p (r u) -> p r u", u=2)
+        def word_tiles(rows, n):
+            words = rows[:].bitcast(F32).rearrange("m (r w) -> m r w", r=n)
+            return [words[:, r, :] for r in range(n)]
+
+        units = []
+
+        def add_units(row_tiles, codes, scales, cols):
+            for c in range(codes.shape[1]):
+                units.append((row_tiles, c, codes[:, c, cols], scales[:, c, cols]))
+
+        add_units(word_tiles(h_raw[0], TILES), h_codes, h_scales, group(0))
+        for c2 in range(F // GROUP):
+            add_units(word_tiles(w1_raw[c2], TILES), w1_codes, w1_scales, group(c2))
+        for half in range(D // GROUP):
+            row_tiles = word_tiles(w2_raw[2 * half], 2) + word_tiles(w2_raw[2 * half + 1], 2)
+            add_units(row_tiles, w2_codes, w2_scales, group(half))
+        add_units(word_tiles(h_raw[1], TILES), h_codes, h_scales, group(1))
+
+        def transposes(unit):
+            row_tiles, c = unit[0], unit[1]
+            banks = []
             for half in range(2):
                 bank = psum.tile([P, 2, 2 * P], F32, tag="bank")
                 for r in range(2):
@@ -84,18 +134,25 @@ def tile_simplifiedretnet_pb_kernel(tc, h_ret, x, W1, b1, W2, b2, ln_g, ln_b, ou
                             row_tiles[2 * half + r][:, first : first + P],
                             ident[:],
                         )
-                nc.scalar.copy(
-                    out=grouped_words[:, half * 2 * P : (half + 1) * 2 * P, :],
-                    in_=bank[:].rearrange("p u r -> p r u"),
-                )
+                banks.append(bank)
+            return banks
+
+        def copy_out(banks, engines):
+            grouped = stage.tile([P, GROUP * PACK], BF16, align_bytes=64, tag="grouped", bufs=5)
+            grouped_words = grouped[:].bitcast(F32).rearrange("p (r u) -> p r u", u=2)
+            for half in range(2):
+                dst = grouped_words[:, half * 2 * P : (half + 1) * 2 * P, :]
+                src = banks[half][:].rearrange("p u r -> p r u")
+                if engines[half] == "vector":
+                    nc.vector.tensor_copy(out=dst, in_=src)
+                else:
+                    nc.scalar.copy(out=dst, in_=src)
+            return grouped
+
+        def quantise(grouped, codes, scales):
             nc.vector.quantize_mx(out=codes.bitcast(FP8X4), scales=scales, in_=grouped[:])
 
-        def word_tiles(rows, n):
-            words = rows[:].bitcast(F32).rearrange("m (r w) -> m r w", r=n)
-            return [words[:, r, :] for r in range(n)]
-
         def first_product(c2, n):
-            tok = slice(n * GROUP, (n + 1) * GROUP)
             g_plain = stage.tile([P, PACK, GROUP], BF16, tag="g_plain")
             for t in range(PACK):
                 rows = slice(c2 * GROUP + t * P, c2 * GROUP + (t + 1) * P)
@@ -105,75 +162,81 @@ def tile_simplifiedretnet_pb_kernel(tc, h_ret, x, W1, b1, W2, b2, ln_g, ln_b, ou
                         out=acc[:],
                         lhsT=w1_codes[:, c, rows].bitcast(FP8X4),
                         lhsT_scale=w1_scales[:, c, rows],
-                        rhs=h_codes[:, c, tok].bitcast(FP8X4),
-                        rhs_scale=h_scales[:, c, tok],
+                        rhs=h_codes[:, c, group(n)].bitcast(FP8X4),
+                        rhs_scale=h_scales[:, c, group(n)],
                         start=(c == 0),
                         stop=(c == H // K_PASS - 1),
                     )
                 j = c2 * PACK + t
                 nc.scalar.activation(
-                    out=g_plain[:, t, :], in_=acc[:], func=ACT.Gelu, bias=b1_f32[:, j : j + 1], scale=1.0
+                    out=g_plain[:, t, :], in_=acc[:], func=ACT.Gelu, bias=b1_cols[:, j : j + 1], scale=1.0
                 )
-            grouped = stage.tile([P, GROUP * PACK], BF16, align_bytes=64, tag="grouped", bufs=3)
+            return g_plain
+
+        def regroup(g_plain):
+            grouped = stage.tile([P, GROUP * PACK], BF16, align_bytes=64, tag="grouped", bufs=5)
             nc.vector.tensor_copy(
                 out=grouped[:].rearrange("p (a i t) -> p a t i", i=4, t=PACK),
                 in_=g_plain[:].rearrange("p t (a i) -> p a t i", i=4),
             )
-            nc.vector.quantize_mx(
-                out=g_codes[:, c2, tok].bitcast(FP8X4), scales=g_scales[:, c2, tok], in_=grouped[:]
-            )
+            return grouped
 
         xb_tiles = []
 
-        def add_bias_to_residual(n):
-            for pair in range(TILES // 2):
+        def add_bias_to_residual(tile_index):
+            n, r = divmod(tile_index, TILES)
+            if r % 2 == 0:
                 xb = raw.tile([P, 2, D], F32, tag="w1_then_xb")
-                for i in range(2):
-                    r = 2 * pair + i
-                    nc.vector.tensor_tensor(
-                        out=xb[:, i, :], in0=x_raw[n][:, r * D : (r + 1) * D], in1=b2_all[:], op=ALU.add
-                    )
-                    xb_tiles.append(xb[:, i, :])
+                xb_tiles.extend([xb[:, 0, :], xb[:, 1, :]])
+            nc.vector.tensor_tensor(
+                out=xb_tiles[tile_index], in0=x_raw[n][:, r * D : (r + 1) * D], in1=b2_all, op=ALU.add
+            )
 
-        def second_product_and_norm(n, r):
+        def second_product(n, r):
             tok = slice(n * GROUP + r * P, n * GROUP + (r + 1) * P)
-            y = stage.tile([P, D], F32, tag="y")
-            sums = stats.tile([P, 2], F32, tag="sums")
+            accs = []
             for half in range(D // GROUP):
-                cols = slice(half * GROUP, (half + 1) * GROUP)
                 acc = psum.tile([P, GROUP], F32, tag="bank")
                 for c in range(F // K_PASS):
                     nc.tensor.matmul_mx(
                         out=acc[:],
                         lhsT=g_codes[:, c, tok].bitcast(FP8X4),
                         lhsT_scale=g_scales[:, c, tok],
-                        rhs=w2_codes[:, c, cols].bitcast(FP8X4),
-                        rhs_scale=w2_scales[:, c, cols],
+                        rhs=w2_codes[:, c, group(half)].bitcast(FP8X4),
+                        rhs_scale=w2_scales[:, c, group(half)],
                         start=(c == 0),
                         stop=(c == F // K_PASS - 1),
                     )
+                accs.append(acc)
+            return accs
+
+        def residual_and_statistics(tile_index, accs):
+            y = stage.tile([P, D], F32, tag="y")
+            sums = stats.tile([P, 2], F32, tag="sums")
+            for half in range(D // GROUP):
                 nc.vector.scalar_tensor_tensor(
-                    out=y[:, cols],
-                    in0=acc[:],
+                    out=y[:, group(half)],
+                    in0=accs[half][:],
                     scalar=1.0,
-                    in1=xb_tiles[n * TILES + r][:, cols],
+                    in1=xb_tiles[tile_index][:, group(half)],
                     op0=ALU.mult,
                     op1=ALU.add,
                     accum_out=sums[:, half : half + 1],
                 )
             neg_mean = stats.tile([P, 2], F32, tag="neg_mean")
-            nc.vector.tensor_scalar(
-                out=neg_mean[:, 0:1], in0=sums[:, 0:1], scalar1=sums[:, 1:2], scalar2=-1.0 / D,
-                op0=ALU.add, op1=ALU.mult,
-            )
-            nc.vector.tensor_scalar(
-                out=neg_mean[:, 1:2], in0=sums[:, 0:1], scalar1=sums[:, 1:2], scalar2=-1.0 / (32.0 * D),
-                op0=ALU.add, op1=ALU.mult,
-            )
+            for column, divisor in enumerate((32.0 * D, 1.0 * D)):
+                nc.vector.tensor_scalar(
+                    out=neg_mean[:, column : column + 1],
+                    in0=sums[:, 0:1],
+                    scalar1=sums[:, 1:2],
+                    scalar2=-1.0 / divisor,
+                    op0=ALU.add,
+                    op1=ALU.mult,
+                )
             squares = stage.tile([P, D], BF16, tag="squares", bufs=1)
             var = stats.tile([P, 1], F32, tag="var")
             nc.scalar.activation(
-                out=squares[:], in_=y[:], func=ACT.Square, bias=neg_mean[:, 1:2], scale=1.0 / 32.0,
+                out=squares[:], in_=y[:], func=ACT.Square, bias=neg_mean[:, 0:1], scale=1.0 / 32.0,
                 accum_out=var[:],
             )
             rstd = stats.tile([P, 2], F32, tag="rstd")
@@ -181,50 +244,55 @@ def tile_simplifiedretnet_pb_kernel(tc, h_ret, x, W1, b1, W2, b2, ln_g, ln_b, ou
                 out=rstd[:, 0:1], in0=var[:], scalar1=1.0, scalar2=LN_EPS, op0=ALU.mult, op1=ALU.add
             )
             nc.gpsimd.tensor_tensor(out=rstd[:, 1:2], in0=rstd[:, 0:1], in1=minus_half[:], op=ALU.pow)
+            return y, neg_mean[:, 1:2], rstd[:, 1:2]
+
+        def centre_and_gain(y, neg_mean):
             normed = stage.tile([P, D], F32, tag="normed", bufs=3)
             nc.vector.scalar_tensor_tensor(
-                out=normed[:], in0=y[:], scalar=neg_mean[:, 0:1], in1=gain_all[:], op0=ALU.add, op1=ALU.mult
+                out=normed[:], in0=y[:], scalar=neg_mean, in1=gain_all, op0=ALU.add, op1=ALU.mult
             )
+            return normed
+
+        def scale_shift_store(tile_index, normed, rstd):
+            n, r = divmod(tile_index, TILES)
             nc.vector.scalar_tensor_tensor(
-                out=normed[:], in0=normed[:], scalar=rstd[:, 1:2], in1=shift_all[:], op0=ALU.mult, op1=ALU.add
+                out=normed[:], in0=normed[:], scalar=rstd, in1=shift_all, op0=ALU.mult, op1=ALU.add
             )
             nc.sync.dma_start(out=out_groups[n][:, r, :], in_=normed[:])
 
-        for n in range(S // GROUP):
-            tok = slice(n * GROUP, (n + 1) * GROUP)
-            for c in range(H // K_PASS):
-                transpose_and_quantise(word_tiles(h_raw[n], TILES), c, h_codes[:, c, tok], h_scales[:, c, tok])
+        RUN = 2
+        waiting = None
+        for i in range(len(units) // RUN):
+            run = units[RUN * i : RUN * (i + 1)]
+            engines = ("scalar", "vector") if i < 2 else ("scalar", "scalar")
+            banks = [transposes(unit) for unit in run]
+            grouped = [copy_out(b, engines) for b in banks]
+            c2 = i - 2
+            g_plain = first_product(c2, 0) if 0 <= c2 < F // GROUP else None
+            if waiting is not None:
+                grouped_g = regroup(waiting[0])
+            quantise(grouped[0], run[0][2], run[0][3])
+            if waiting is not None:
+                quantise(grouped_g, waiting[1], waiting[2])
+            quantise(grouped[1], run[1][2], run[1][3])
+            if c2 >= 0:
+                add_bias_to_residual(c2)
+            waiting = None
+            if g_plain is not None:
+                waiting = (g_plain, g_codes[:, c2, group(0)], g_scales[:, c2, group(0)])
 
-        b2_all = keep.tile([P, D], BF16)
-        nc.sync.dma_start(out=b2_all[:], in_=b2.partition_broadcast(P))
-        x_raw = [load_tokens(x_groups[0])]
-        w2_pairs = W2.rearrange("(n r m) k -> n m r k", r=2, m=P)
-        w2_raw = []
-        for n in range(D // (2 * P)):
-            rows = raw.tile([P, 2 * F], BF16, tag="w2")
-            nc.sync.dma_start(out=rows[:].rearrange("m (r k) -> m r k", r=2), in_=w2_pairs[n])
-            w2_raw.append(rows)
-        x_raw.append(load_tokens(x_groups[1]))
-        gain_all = keep.tile([P, D], BF16)
-        nc.sync.dma_start(out=gain_all[:], in_=ln_g.partition_broadcast(P))
-        shift_all = keep.tile([P, D], BF16)
-        nc.sync.dma_start(out=shift_all[:], in_=ln_b.partition_broadcast(P))
-
-        for c2 in range(F // GROUP):
-            rows = slice(c2 * GROUP, (c2 + 1) * GROUP)
-            for c in range(H // K_PASS):
-                transpose_and_quantise(word_tiles(w1_raw[c2], TILES), c, w1_codes[:, c, rows], w1_scales[:, c, rows])
-            first_product(c2, 0)
-        add_bias_to_residual(0)
-        for half in range(D // GROUP):
-            cols = slice(half * GROUP, (half + 1) * GROUP)
-            row_tiles = word_tiles(w2_raw[2 * half], 2) + word_tiles(w2_raw[2 * half + 1], 2)
-            for c in range(F // K_PASS):
-                transpose_and_quantise(row_tiles, c, w2_codes[:, c, cols], w2_scales[:, c, cols])
-        for r in range(TILES):
-            second_product_and_norm(0, r)
-        for c2 in range(F // GROUP):
-            first_product(c2, 1)
-        add_bias_to_residual(1)
-        for r in range(TILES):
-            second_product_and_norm(1, r)
+        unfinished = None
+        for step in range(S // P):
+            if step < F // GROUP:
+                g_plain = first_product(step, 1)
+            accs = second_product(step // TILES, step % TILES)
+            y, neg_mean, rstd = residual_and_statistics(step, accs)
+            if step < F // GROUP:
+                grouped_g = regroup(g_plain)
+            if unfinished is not None:
+                scale_shift_store(unfinished[0], unfinished[1], unfinished[2])
+            normed = centre_and_gain(y, neg_mean)
+            unfinished = (step, normed, rstd)
+            if step < F // GROUP:
+                quantise(grouped_g, g_codes[:, step, group(1)], g_scales[:, step, group(1)])
+        scale_shift_store(unfinished[0], unfinished[1], unfinished[2])

@@ -32,48 +32,63 @@ def tile_simplifiedretnet_pb_kernel(tc, h_ret, x, W1, b1, W2, b2, ln_g, ln_b, ou
         psum = ctx.enter_context(tc.psum_pool(name="psum", bufs=8))
         ctx.enter_context(tc.manual_schedule())
 
-        row0 = keep.tile([P, 3 * D], BF16)
-        nc.vector.memset(row0[:].bitcast(F32), 0.0)
-        for i, vector in enumerate((b2, ln_g, ln_b)):
-            nc.scalar.dma_start(out=row0[0:1, i * D : (i + 1) * D], in_=vector.unsqueeze(0))
-        b1_cols = keep.tile([P, F // P], BF16)
-        nc.scalar.dma_start(
-            out=b1_cols[:].rearrange("m (a e) -> m a e", e=2),
-            in_=b1.rearrange("(a m e) -> m a e", m=P, e=2),
-        )
-
         tokens = "(n m r) k -> n m (r k)"
         h_groups = h_ret.flatten_outer_dims().rearrange(tokens, m=P, r=TILES)
         x_groups = x.flatten_outer_dims().rearrange(tokens, m=P, r=TILES)
         out_groups = out.flatten_outer_dims().rearrange("(n m r) d -> n m r d", m=P, r=TILES)
-        w1_groups = W1.rearrange("(c u m e) k -> c m u (e k)", u=2, m=P, e=2)
+        w1_groups = W1.rearrange("(c u m e) k -> c u m (e k)", u=2, m=P, e=2)
         w2_pairs = W2.rearrange("(n r m) k -> n m r k", r=2, m=P)
 
-        def load_tokens(dram_rows, tag):
-            rows = raw.tile([P, TILES * H], BF16, tag=tag, bufs=2)
-            nc.sync.dma_start(out=rows[:], in_=dram_rows)
-            return rows
+        h_raw, w1_raw, w2_raw, x_raw = [], [], [], []
+
+        def load_h(n):
+            rows = raw.tile([P, TILES * H], BF16, tag="h", bufs=2)
+            for half in range(2):
+                cols = slice(half * 2 * H, (half + 1) * 2 * H)
+                nc.sync.dma_start(out=rows[:, cols], in_=h_groups[n][:, cols])
+            h_raw.append(rows)
+
+        def load_x(n):
+            rows = raw.tile([P, TILES * D], BF16, tag="x", bufs=2)
+            nc.sync.dma_start(out=rows[:], in_=x_groups[n])
+            x_raw.append(rows)
 
         def load_w1(c):
             rows = raw.tile([P, TILES * H], BF16, tag="w1_then_xb")
-            nc.sync.dma_start(out=rows[:].rearrange("m (u k) -> m u k", u=2), in_=w1_groups[c])
-            return rows
+            for u in range(2):
+                nc.sync.dma_start(out=rows[:, u * 2 * H : (u + 1) * 2 * H], in_=w1_groups[c, u])
+            w1_raw.append(rows)
 
         def load_w2(n):
             rows = raw.tile([P, 2 * F], BF16, tag="w2")
             nc.sync.dma_start(out=rows[:].rearrange("m (r k) -> m r k", r=2), in_=w2_pairs[n])
-            return rows
+            w2_raw.append(rows)
 
-        h_raw = [load_tokens(h_groups[0], "h")]
-        w1_raw = [load_w1(0), load_w1(1)]
-        x_raw = [load_tokens(x_groups[0], "x")]
-        w1_raw.extend([load_w1(2), load_w1(3)])
-        x_raw.append(load_tokens(x_groups[1], "x"))
-        w2_raw = [load_w2(n) for n in range(D // (2 * P))]
-        h_raw.append(load_tokens(h_groups[1], "h"))
+        b1_rows = keep.tile([P, P], F32)
+        nc.gpsimd.memset(b1_rows[:], 0.0)
+        row0 = keep.tile([P, 3 * D], BF16)
+        nc.gpsimd.memset(row0[:].bitcast(F32), 0.0)
+        load_h(0)
+        load_w1(0)
+        nc.scalar.dma_start(
+            out=b1_rows[0 : F // (2 * P), :].bitcast(BF16), in_=b1.rearrange("(a w) -> a w", w=2 * P)
+        )
+        for i, vector in enumerate((b2, ln_g, ln_b)):
+            nc.scalar.dma_start(out=row0[0:1, i * D : (i + 1) * D], in_=vector.unsqueeze(0))
+        for c in range(1, F // GROUP):
+            load_w1(c)
+        load_w2(0)
+        load_w2(1)
+        load_h(1)
+        load_x(0)
+        load_w2(2)
+        load_w2(3)
+        load_x(1)
 
         ident = keep.tile([P, P], F32)
         make_identity(nc, ident[:])
+        ident_bf16 = keep.tile([P, P], BF16)
+        nc.vector.tensor_copy(out=ident_bf16[:], in_=ident[:])
         minus_half = keep.tile([P, 1], F32)
         nc.vector.memset(minus_half[:], -0.5)
         ones = keep.tile([P, P], BF16)
@@ -84,15 +99,22 @@ def tile_simplifiedretnet_pb_kernel(tc, h_ret, x, W1, b1, W2, b2, ln_g, ln_b, ou
         def group(n):
             return slice(n * GROUP, (n + 1) * GROUP)
 
+        b1_words = keep.tile([P, F // (2 * P)], F32)
+        b1_cols = b1_words[:].bitcast(BF16)
         repeated = keep.tile([P, 3 * D], BF16)
-        for j in range(3 * D // GROUP):
-            acc = psum.tile([P, GROUP], F32, tag="bank")
-            nc.tensor.matmul(out=acc[:], lhsT=ones[:], rhs=row0[:, group(j)], start=True, stop=True)
-            if j % 2 == 0:
-                nc.vector.tensor_copy(out=repeated[:, group(j)], in_=acc[:])
-            else:
-                nc.scalar.copy(out=repeated[:, group(j)], in_=acc[:])
         b2_all, gain_all, shift_all = [repeated[:, i * D : (i + 1) * D] for i in range(3)]
+
+        def spread_b1():
+            bank = psum.tile([P, P], F32, tag="bank")
+            nc.tensor.transpose(bank[:], b1_rows[:], ident[:])
+            nc.scalar.copy(out=b1_words[:], in_=bank[:, : F // (2 * P)])
+
+        def repeat_vector(i):
+            bank = psum.tile([P, D], BF16, tag="bank")
+            for half in range(D // GROUP):
+                cols = slice(i * D + half * GROUP, i * D + (half + 1) * GROUP)
+                nc.tensor.matmul(out=bank[:, group(half)], lhsT=ones[:], rhs=row0[:, cols], start=True, stop=True)
+            nc.scalar.copy(out=repeated[:, i * D : (i + 1) * D], in_=bank[:])
 
         h_codes = keep.tile([P, H // K_PASS, S], U32, align_bytes=64)
         h_scales = keep.tile([P, H // K_PASS, S], U8, align_bytes=64)
@@ -107,63 +129,60 @@ def tile_simplifiedretnet_pb_kernel(tc, h_ret, x, W1, b1, W2, b2, ln_g, ln_b, ou
             words = rows[:].bitcast(F32).rearrange("m (r w) -> m r w", r=n)
             return [words[:, r, :] for r in range(n)]
 
-        units = []
+        def units_of(row_tiles, codes, scales, cols):
+            return [(row_tiles, c, codes[:, c, cols], scales[:, c, cols]) for c in range(codes.shape[1])]
 
-        def add_units(row_tiles, codes, scales, cols):
-            for c in range(codes.shape[1]):
-                units.append((row_tiles, c, codes[:, c, cols], scales[:, c, cols]))
+        def h_units(n):
+            return units_of(word_tiles(h_raw[n], TILES), h_codes, h_scales, group(n))
 
-        add_units(word_tiles(h_raw[0], TILES), h_codes, h_scales, group(0))
-        for c2 in range(F // GROUP):
-            add_units(word_tiles(w1_raw[c2], TILES), w1_codes, w1_scales, group(c2))
-        for half in range(D // GROUP):
+        def w1_units(c2):
+            return units_of(word_tiles(w1_raw[c2], TILES), w1_codes, w1_scales, group(c2))
+
+        def w2_units(half):
             row_tiles = word_tiles(w2_raw[2 * half], 2) + word_tiles(w2_raw[2 * half + 1], 2)
-            add_units(row_tiles, w2_codes, w2_scales, group(half))
-        add_units(word_tiles(h_raw[1], TILES), h_codes, h_scales, group(1))
+            return units_of(row_tiles, w2_codes, w2_scales, group(half))
 
-        def transposes(unit):
-            row_tiles, c = unit[0], unit[1]
-            banks = []
+        def transpose_run(run, engines):
+            grouped = [stage.tile([P, GROUP * PACK], BF16, align_bytes=64, tag="grouped", bufs=5, name="grouped") for unit in run]
+            which = 0
             for half in range(2):
-                bank = psum.tile([P, 2, 2 * P], F32, tag="bank")
-                for r in range(2):
-                    for u in range(2):
-                        first = (2 * c + u) * P
-                        nc.tensor.transpose(
-                            bank[:, u, r * P : (r + 1) * P],
-                            row_tiles[2 * half + r][:, first : first + P],
-                            ident[:],
-                        )
-                banks.append(bank)
-            return banks
-
-        def copy_out(banks, engines):
-            grouped = stage.tile([P, GROUP * PACK], BF16, align_bytes=64, tag="grouped", bufs=5)
-            grouped_words = grouped[:].bitcast(F32).rearrange("p (r u) -> p r u", u=2)
-            for half in range(2):
-                dst = grouped_words[:, half * 2 * P : (half + 1) * 2 * P, :]
-                src = banks[half][:].rearrange("p u r -> p r u")
-                if engines[half] == "vector":
-                    nc.vector.tensor_copy(out=dst, in_=src)
-                else:
-                    nc.scalar.copy(out=dst, in_=src)
+                for unit, dst_tile in zip(run, grouped):
+                    row_tiles, c = unit[0], unit[1]
+                    bank = psum.tile([P, 2, 2 * P], F32, tag="bank")
+                    for r in range(2):
+                        for u in range(2):
+                            first = (2 * c + u) * P
+                            nc.tensor.transpose(
+                                bank[:, u, r * P : (r + 1) * P],
+                                row_tiles[2 * half + r][:, first : first + P],
+                                ident[:],
+                            )
+                    words = dst_tile[:].bitcast(F32).rearrange("p (r u) -> p r u", u=2)
+                    dst = words[:, half * 2 * P : (half + 1) * 2 * P, :]
+                    src = bank[:].rearrange("p u r -> p r u")
+                    if engines[which] == "v":
+                        nc.vector.tensor_copy(out=dst, in_=src)
+                    else:
+                        nc.scalar.copy(out=dst, in_=src)
+                    which += 1
             return grouped
 
         def quantise(grouped, codes, scales):
             nc.vector.quantize_mx(out=codes.bitcast(FP8X4), scales=scales, in_=grouped[:])
 
-        def first_product(c2, n):
-            g_plain = stage.tile([P, PACK, GROUP], BF16, tag="g_plain")
+        def first_product(c2, tok):
+            width = tok.stop - tok.start
+            g_plain = stage.tile([P, PACK, width], BF16, tag="g_plain", bufs=3)
             for t in range(PACK):
                 rows = slice(c2 * GROUP + t * P, c2 * GROUP + (t + 1) * P)
-                acc = psum.tile([P, GROUP], F32, tag="bank")
+                acc = psum.tile([P, width], F32, tag="bank")
                 for c in range(H // K_PASS):
                     nc.tensor.matmul_mx(
                         out=acc[:],
                         lhsT=w1_codes[:, c, rows].bitcast(FP8X4),
                         lhsT_scale=w1_scales[:, c, rows],
-                        rhs=h_codes[:, c, group(n)].bitcast(FP8X4),
-                        rhs_scale=h_scales[:, c, group(n)],
+                        rhs=h_codes[:, c, tok].bitcast(FP8X4),
+                        rhs_scale=h_scales[:, c, tok],
                         start=(c == 0),
                         stop=(c == H // K_PASS - 1),
                     )
@@ -171,26 +190,43 @@ def tile_simplifiedretnet_pb_kernel(tc, h_ret, x, W1, b1, W2, b2, ln_g, ln_b, ou
                 nc.scalar.activation(
                     out=g_plain[:, t, :], in_=acc[:], func=ACT.Gelu, bias=b1_cols[:, j : j + 1], scale=1.0
                 )
-            return g_plain
+            return g_plain, c2, tok
 
         def regroup(g_plain):
-            grouped = stage.tile([P, GROUP * PACK], BF16, align_bytes=64, tag="grouped", bufs=5)
+            grouped = stage.tile([P, g_plain.shape[1] * g_plain.shape[2]], BF16, align_bytes=64, tag="grouped", bufs=5)
             nc.vector.tensor_copy(
                 out=grouped[:].rearrange("p (a i t) -> p a t i", i=4, t=PACK),
                 in_=g_plain[:].rearrange("p t (a i) -> p a t i", i=4),
             )
             return grouped
 
-        xb_tiles = []
+        xb_tiles = [None] * (S // P)
 
-        def add_bias_to_residual(tile_index):
-            n, r = divmod(tile_index, TILES)
-            if r % 2 == 0:
+        def xb_tile(tile_index):
+            if xb_tiles[tile_index] is None:
                 xb = raw.tile([P, 2, D], F32, tag="w1_then_xb")
-                xb_tiles.extend([xb[:, 0, :], xb[:, 1, :]])
+                xb_tiles[tile_index] = xb[:, 0, :]
+                xb_tiles[tile_index + 1] = xb[:, 1, :]
+            return xb_tiles[tile_index]
+
+        def residual_vector(tile_index):
+            n, r = divmod(tile_index, TILES)
             nc.vector.tensor_tensor(
-                out=xb_tiles[tile_index], in0=x_raw[n][:, r * D : (r + 1) * D], in1=b2_all, op=ALU.add
+                out=xb_tile(tile_index), in0=x_raw[n][:, r * D : (r + 1) * D], in1=b2_all, op=ALU.add
             )
+
+        def residual_tensor(tile_index):
+            n, r = divmod(tile_index, TILES)
+            xb = xb_tile(tile_index)
+            for half in range(D // GROUP):
+                cols = slice(half * GROUP, (half + 1) * GROUP)
+                bank = psum.tile([P, GROUP], F32, tag="bank")
+                nc.tensor.matmul(
+                    out=bank[:], lhsT=ident_bf16[:], rhs=x_raw[n][:, r * D + half * GROUP : r * D + (half + 1) * GROUP],
+                    start=True, stop=False,
+                )
+                nc.tensor.matmul(out=bank[:], lhsT=ones[:], rhs=row0[:, cols], start=False, stop=True)
+                nc.scalar.copy(out=xb[:, cols], in_=bank[:])
 
         def second_product(n, r):
             tok = slice(n * GROUP + r * P, n * GROUP + (r + 1) * P)
@@ -210,7 +246,7 @@ def tile_simplifiedretnet_pb_kernel(tc, h_ret, x, W1, b1, W2, b2, ln_g, ln_b, ou
                 accs.append(acc)
             return accs
 
-        def residual_and_statistics(tile_index, accs):
+        def add_residual(tile_index, accs):
             y = stage.tile([P, D], F32, tag="y")
             sums = stats.tile([P, 2], F32, tag="sums")
             for half in range(D // GROUP):
@@ -223,76 +259,104 @@ def tile_simplifiedretnet_pb_kernel(tc, h_ret, x, W1, b1, W2, b2, ln_g, ln_b, ou
                     op1=ALU.add,
                     accum_out=sums[:, half : half + 1],
                 )
-            neg_mean = stats.tile([P, 2], F32, tag="neg_mean")
-            for column, divisor in enumerate((32.0 * D, 1.0 * D)):
-                nc.vector.tensor_scalar(
-                    out=neg_mean[:, column : column + 1],
-                    in0=sums[:, 0:1],
-                    scalar1=sums[:, 1:2],
-                    scalar2=-1.0 / divisor,
-                    op0=ALU.add,
-                    op1=ALU.mult,
-                )
+            return y, sums
+
+        def negative_mean(sums):
+            neg_mean = stats.tile([P, 1], F32, tag="neg_mean")
+            nc.vector.tensor_scalar(
+                out=neg_mean[:], in0=sums[:, 0:1], scalar1=sums[:, 1:2], scalar2=-1.0 / D, op0=ALU.add, op1=ALU.mult
+            )
+            return neg_mean
+
+        def inverse_deviation(y, neg_mean):
             squares = stage.tile([P, D], BF16, tag="squares", bufs=1)
             var = stats.tile([P, 1], F32, tag="var")
             nc.scalar.activation(
-                out=squares[:], in_=y[:], func=ACT.Square, bias=neg_mean[:, 0:1], scale=1.0 / 32.0,
-                accum_out=var[:],
+                out=squares[:], in_=y[:], func=ACT.Square, bias=neg_mean[:], scale=1.0, accum_out=var[:]
             )
             rstd = stats.tile([P, 2], F32, tag="rstd")
             nc.gpsimd.tensor_scalar(
-                out=rstd[:, 0:1], in0=var[:], scalar1=1.0, scalar2=LN_EPS, op0=ALU.mult, op1=ALU.add
+                out=rstd[:, 0:1], in0=var[:], scalar1=1.0 / D, scalar2=LN_EPS, op0=ALU.mult, op1=ALU.add
             )
             nc.gpsimd.tensor_tensor(out=rstd[:, 1:2], in0=rstd[:, 0:1], in1=minus_half[:], op=ALU.pow)
-            return y, neg_mean[:, 1:2], rstd[:, 1:2]
+            return rstd[:, 1:2]
 
         def centre_and_gain(y, neg_mean):
             normed = stage.tile([P, D], F32, tag="normed", bufs=3)
             nc.vector.scalar_tensor_tensor(
-                out=normed[:], in0=y[:], scalar=neg_mean, in1=gain_all, op0=ALU.add, op1=ALU.mult
+                out=normed[:], in0=y[:], scalar=neg_mean[:], in1=gain_all, op0=ALU.add, op1=ALU.mult
             )
             return normed
 
-        def scale_shift_store(tile_index, normed, rstd):
+        def scale_shift_store(tile_index, normed, rstd, half):
             n, r = divmod(tile_index, TILES)
+            cols = group(half)
             nc.vector.scalar_tensor_tensor(
-                out=normed[:], in0=normed[:], scalar=rstd, in1=shift_all, op0=ALU.mult, op1=ALU.add
+                out=normed[:, cols], in0=normed[:, cols], scalar=rstd, in1=shift_all[:, cols], op0=ALU.mult, op1=ALU.add
             )
-            nc.sync.dma_start(out=out_groups[n][:, r, :], in_=normed[:])
+            nc.sync.dma_start(out=out_groups[n][:, r, cols], in_=normed[:, cols])
 
-        RUN = 2
-        waiting = None
-        for i in range(len(units) // RUN):
-            run = units[RUN * i : RUN * (i + 1)]
-            engines = ("scalar", "vector") if i < 2 else ("scalar", "scalar")
-            banks = [transposes(unit) for unit in run]
-            grouped = [copy_out(b, engines) for b in banks]
-            c2 = i - 2
-            g_plain = first_product(c2, 0) if 0 <= c2 < F // GROUP else None
-            if waiting is not None:
-                grouped_g = regroup(waiting[0])
-            quantise(grouped[0], run[0][2], run[0][3])
-            if waiting is not None:
-                quantise(grouped_g, waiting[1], waiting[2])
-            quantise(grouped[1], run[1][2], run[1][3])
-            if c2 >= 0:
-                add_bias_to_residual(c2)
-            waiting = None
-            if g_plain is not None:
-                waiting = (g_plain, g_codes[:, c2, group(0)], g_scales[:, c2, group(0)])
+        waiting = []
 
+        def start_grouping():
+            todo = [(regroup(g), g_codes[:, c2, tok], g_scales[:, c2, tok]) for g, c2, tok in waiting]
+            waiting.clear()
+            return todo
+
+        def step(run=(), engines="", product=None, extra=()):
+            grouped = transpose_run(run, engines) if run else []
+            new = first_product(*product) if product else None
+            todo = start_grouping()
+            for unit, tile in zip(run, grouped):
+                todo.insert(0, (tile, unit[2], unit[3]))
+            for t in extra:
+                residual_vector(t)
+            for item in todo:
+                quantise(*item)
+            if product:
+                waiting.append(new)
+
+        def tokens_of(first, count):
+            return slice(first * P, (first + count) * P)
+
+        G0, G1 = tokens_of(0, 4), tokens_of(4, 4)
+        w2a, w2b = w2_units(0), w2_units(1)
+        step(h_units(0), "svsv")
+        spread_b1()
+        step(w1_units(0), "svsv")
+        step(w1_units(1), "sssv", (0, G0))
+        repeat_vector(0)
+        step(w1_units(2), "sssv", (1, G0))
+        step(w1_units(3), "sssv", (2, G0))
+        step(h_units(1), "sssv", (3, G0), ())
+        step(w2a[0:2], "sssv", (0, G1), (0,))
+        step(w2a[2:4], "sssv", None, (1,))
+        step(w2b[0:2], "sssv", (1, G1), ())
+        repeat_vector(1)
+        step(w2b[2:4], "sssv", (2, G1), ())
+        repeat_vector(2)
+
+        step()
+
+        first_of_step = {0: [(3, tokens_of(4, 4))]}
         unfinished = None
-        for step in range(S // P):
-            if step < F // GROUP:
-                g_plain = first_product(step, 1)
-            accs = second_product(step // TILES, step % TILES)
-            y, neg_mean, rstd = residual_and_statistics(step, accs)
-            if step < F // GROUP:
-                grouped_g = regroup(g_plain)
+        for t in range(S // P):
+            for c2, tok in first_of_step.get(t, ()):
+                waiting.append(first_product(c2, tok))
+            accs = second_product(t // TILES, t % TILES)
+            if t + 2 in (2, 3, 4, 5, 6, 7,):
+                residual_tensor(t + 2)
+            y, sums = add_residual(t, accs)
+            todo = start_grouping()
             if unfinished is not None:
-                scale_shift_store(unfinished[0], unfinished[1], unfinished[2])
+                scale_shift_store(*unfinished, 0)
+            neg_mean = negative_mean(sums)
+            rstd = inverse_deviation(y, neg_mean)
+            if unfinished is not None:
+                scale_shift_store(*unfinished, 1)
+            for item in todo:
+                quantise(*item)
             normed = centre_and_gain(y, neg_mean)
-            unfinished = (step, normed, rstd)
-            if step < F // GROUP:
-                quantise(grouped_g, g_codes[:, step, group(1)], g_scales[:, step, group(1)])
-        scale_shift_store(unfinished[0], unfinished[1], unfinished[2])
+            unfinished = (t, normed, rstd)
+        scale_shift_store(*unfinished, 0)
+        scale_shift_store(*unfinished, 1)

@@ -77,12 +77,10 @@ def tile_simplifiedretnet_pb_kernel(tc, h_ret, x, W1, b1, W2, b2, ln_g, ln_b, ou
             nc.scalar.dma_start(out=row0[0:1, i * D : (i + 1) * D], in_=vector.unsqueeze(0))
         for c in range(1, F // GROUP):
             load_w1(c)
-        load_w2(0)
-        load_w2(1)
-        load_h(1)
+        for n in range(D // (2 * P)):
+            load_w2(n)
         load_x(0)
-        load_w2(2)
-        load_w2(3)
+        load_h(1)
         load_x(1)
 
         ident = keep.tile([P, P], F32)
@@ -175,10 +173,12 @@ def tile_simplifiedretnet_pb_kernel(tc, h_ret, x, W1, b1, W2, b2, ln_g, ln_b, ou
             g_plain = stage.tile([P, PACK, width], BF16, tag="g_plain", bufs=3)
             for t in range(PACK):
                 rows = slice(c2 * GROUP + t * P, c2 * GROUP + (t + 1) * P)
-                acc = psum.tile([P, width], F32, tag="bank")
+                if t * width % GROUP == 0:
+                    bank = psum.tile([P, GROUP], F32, tag="bank")
+                acc = bank[:, t * width % GROUP : t * width % GROUP + width]
                 for c in range(H // K_PASS):
                     nc.tensor.matmul_mx(
-                        out=acc[:],
+                        out=acc,
                         lhsT=w1_codes[:, c, rows].bitcast(FP8X4),
                         lhsT_scale=w1_scales[:, c, rows],
                         rhs=h_codes[:, c, tok].bitcast(FP8X4),
@@ -188,7 +188,7 @@ def tile_simplifiedretnet_pb_kernel(tc, h_ret, x, W1, b1, W2, b2, ln_g, ln_b, ou
                     )
                 j = c2 * PACK + t
                 nc.scalar.activation(
-                    out=g_plain[:, t, :], in_=acc[:], func=ACT.Gelu, bias=b1_cols[:, j : j + 1], scale=1.0
+                    out=g_plain[:, t, :], in_=acc, func=ACT.Gelu, bias=b1_cols[:, j : j + 1], scale=1.0
                 )
             return g_plain, c2, tok
 
@@ -247,7 +247,7 @@ def tile_simplifiedretnet_pb_kernel(tc, h_ret, x, W1, b1, W2, b2, ln_g, ln_b, ou
             return accs
 
         def add_residual(tile_index, accs):
-            y = stage.tile([P, D], F32, tag="y")
+            y = stage.tile([P, D], F32, tag="y", bufs=2)
             sums = stats.tile([P, 2], F32, tag="sums")
             for half in range(D // GROUP):
                 nc.vector.scalar_tensor_tensor(
@@ -319,43 +319,46 @@ def tile_simplifiedretnet_pb_kernel(tc, h_ret, x, W1, b1, W2, b2, ln_g, ln_b, ou
         def tokens_of(first, count):
             return slice(first * P, (first + count) * P)
 
-        G0, G1 = tokens_of(0, 4), tokens_of(4, 4)
+        A, B, C, E = [tokens_of(2 * i, 2) for i in range(4)]
         w2a, w2b = w2_units(0), w2_units(1)
         step(h_units(0), "svsv")
-        spread_b1()
         step(w1_units(0), "svsv")
-        step(w1_units(1), "sssv", (0, G0))
+        spread_b1()
+        step(w1_units(1), "sssv", (0, A))
+        step(w1_units(2), "sssv", (1, A))
+        step(w1_units(3), "sssv", (2, A))
         repeat_vector(0)
-        step(w1_units(2), "sssv", (1, G0))
-        step(w1_units(3), "sssv", (2, G0))
-        step(h_units(1), "sssv", (3, G0), ())
-        step(w2a[0:2], "sssv", (0, G1), (0,))
-        step(w2a[2:4], "sssv", None, (1,))
-        step(w2b[0:2], "sssv", (1, G1), ())
+        step(w2a[0:2], "sssv", (3, A), ())
+        step(w2a[2:4], "sssv", None, ())
+        step(w2b[0:2], "sssv", (0, B), (0,))
         repeat_vector(1)
-        step(w2b[2:4], "sssv", (2, G1), ())
+        step(w2b[2:4], "ssss", (1, B), (1,))
         repeat_vector(2)
 
-        step()
-
-        first_of_step = {0: [(3, tokens_of(4, 4))]}
+        products = {0: [(2, B), (3, B)], 1: [(0, C), (1, C)], 2: [(2, C), (3, C)], 3: [(0, E), (1, E)], 4: [(2, E), (3, E)]}
         unfinished = None
         for t in range(S // P):
-            for c2, tok in first_of_step.get(t, ()):
-                waiting.append(first_product(c2, tok))
             accs = second_product(t // TILES, t % TILES)
-            if t + 2 in (2, 3, 4, 5, 6, 7,):
-                residual_tensor(t + 2)
-            y, sums = add_residual(t, accs)
+            if t == 0:
+                run = h_units(1)
+                grouped = transpose_run(run, "ssss")
             todo = start_grouping()
-            if unfinished is not None:
-                scale_shift_store(*unfinished, 0)
+            y, sums = add_residual(t, accs)
+            for c2, tok in products.get(t, ()):
+                waiting.append(first_product(c2, tok))
+            if t + 1 not in (0, 1, S // P):
+                residual_tensor(t + 1)
+            if t == 0:
+                todo.extend([(tile, unit[2], unit[3]) for unit, tile in zip(run, grouped)])
+            if todo:
+                quantise(*todo.pop(0))
             neg_mean = negative_mean(sums)
             rstd = inverse_deviation(y, neg_mean)
+            while todo:
+                quantise(*todo.pop(0))
             if unfinished is not None:
+                scale_shift_store(*unfinished, 0)
                 scale_shift_store(*unfinished, 1)
-            for item in todo:
-                quantise(*item)
             normed = centre_and_gain(y, neg_mean)
             unfinished = (t, normed, rstd)
         scale_shift_store(*unfinished, 0)

@@ -171,25 +171,27 @@ def tile_simplifiedretnet_pb_kernel(tc, h_ret, x, W1, b1, W2, b2, ln_g, ln_b, ou
         def first_product(c2, tok):
             width = tok.stop - tok.start
             g_plain = stage.tile([P, PACK, width], BF16, tag="g_plain", bufs=3)
-            for t in range(PACK):
-                rows = slice(c2 * GROUP + t * P, c2 * GROUP + (t + 1) * P)
-                if t * width % GROUP == 0:
-                    bank = psum.tile([P, GROUP], F32, tag="bank")
-                acc = bank[:, t * width % GROUP : t * width % GROUP + width]
-                for c in range(H // K_PASS):
-                    nc.tensor.matmul_mx(
-                        out=acc,
-                        lhsT=w1_codes[:, c, rows].bitcast(FP8X4),
-                        lhsT_scale=w1_scales[:, c, rows],
-                        rhs=h_codes[:, c, tok].bitcast(FP8X4),
-                        rhs_scale=h_scales[:, c, tok],
-                        start=(c == 0),
-                        stop=(c == H // K_PASS - 1),
+            share = GROUP // width
+            for first in range(0, PACK, share):
+                bank = psum.tile([P, share, width], F32, tag="bank")
+                for i in range(share):
+                    t = first + i
+                    rows = slice(c2 * GROUP + t * P, c2 * GROUP + (t + 1) * P)
+                    for c in range(H // K_PASS):
+                        nc.tensor.matmul_mx(
+                            out=bank[:, i, :],
+                            lhsT=w1_codes[:, c, rows].bitcast(FP8X4),
+                            lhsT_scale=w1_scales[:, c, rows],
+                            rhs=h_codes[:, c, tok].bitcast(FP8X4),
+                            rhs_scale=h_scales[:, c, tok],
+                            start=(c == 0),
+                            stop=(c == H // K_PASS - 1),
+                        )
+                for i in range(share):
+                    j = c2 * PACK + first + i
+                    nc.scalar.activation(
+                        out=g_plain[:, first + i, :], in_=bank[:, i, :], func=ACT.Gelu, bias=b1_cols[:, j : j + 1], scale=1.0
                     )
-                j = c2 * PACK + t
-                nc.scalar.activation(
-                    out=g_plain[:, t, :], in_=acc, func=ACT.Gelu, bias=b1_cols[:, j : j + 1], scale=1.0
-                )
             return g_plain, c2, tok
 
         def regroup(g_plain):

@@ -39,6 +39,14 @@ def tile_simplifiedretnet_pb_kernel(tc, h_ret, x, W1, b1, W2, b2, ln_g, ln_b, ou
         w1_groups = W1.rearrange("(c u m e) k -> c u m (e k)", u=2, m=P, e=2)
         w2_pairs = W2.rearrange("(n r m) k -> n m r k", r=2, m=P)
 
+        ident = keep.tile([P, P], F32)
+        make_identity(nc, ident[:])
+        ident_bf16 = keep.tile([P, P], BF16)
+        minus_half = keep.tile([P, 1], F32)
+        nc.vector.memset(minus_half[:], -0.5)
+        ones = keep.tile([P, P], BF16)
+        nc.vector.memset(ones[:], 1.0)
+
         h_raw, w1_raw, w2_raw, x_raw = [], [], [], []
 
         def load_h(n):
@@ -65,9 +73,9 @@ def tile_simplifiedretnet_pb_kernel(tc, h_ret, x, W1, b1, W2, b2, ln_g, ln_b, ou
             w2_raw.append(rows)
 
         b1_rows = keep.tile([P, P], F32)
-        nc.gpsimd.memset(b1_rows[:], 0.0)
+        nc.vector.memset(b1_rows[:], 0.0)
         row0 = keep.tile([P, 3 * D], BF16)
-        nc.gpsimd.memset(row0[:].bitcast(F32), 0.0)
+        nc.vector.memset(row0[:].bitcast(F32), 0.0)
         load_h(0)
         load_w1(0)
         nc.scalar.dma_start(
@@ -75,6 +83,8 @@ def tile_simplifiedretnet_pb_kernel(tc, h_ret, x, W1, b1, W2, b2, ln_g, ln_b, ou
         )
         for i, vector in enumerate((b2, ln_g, ln_b)):
             nc.scalar.dma_start(out=row0[0:1, i * D : (i + 1) * D], in_=vector.unsqueeze(0))
+        warm = keep.tile([P, 1], F32)
+        nc.scalar.activation(out=warm[:], in_=minus_half[:], func=ACT.Gelu)
         for c in range(1, F // GROUP):
             load_w1(c)
         for n in range(D // (2 * P)):
@@ -83,16 +93,7 @@ def tile_simplifiedretnet_pb_kernel(tc, h_ret, x, W1, b1, W2, b2, ln_g, ln_b, ou
         load_h(1)
         load_x(1)
 
-        ident = keep.tile([P, P], F32)
-        make_identity(nc, ident[:])
-        ident_bf16 = keep.tile([P, P], BF16)
         nc.vector.tensor_copy(out=ident_bf16[:], in_=ident[:])
-        minus_half = keep.tile([P, 1], F32)
-        nc.vector.memset(minus_half[:], -0.5)
-        ones = keep.tile([P, P], BF16)
-        nc.vector.memset(ones[:], 1.0)
-        warm = keep.tile([P, 1], F32)
-        nc.scalar.activation(out=warm[:], in_=minus_half[:], func=ACT.Gelu)
 
         def group(n):
             return slice(n * GROUP, (n + 1) * GROUP)
@@ -321,21 +322,21 @@ def tile_simplifiedretnet_pb_kernel(tc, h_ret, x, W1, b1, W2, b2, ln_g, ln_b, ou
         def tokens_of(first, count):
             return slice(first * P, (first + count) * P)
 
-        A, B, C, E = [tokens_of(2 * i, 2) for i in range(4)]
+        A, B, C, E = tokens_of(0, 2), tokens_of(2, 2), tokens_of(4, 2), tokens_of(6, 2)
         w2a, w2b = w2_units(0), w2_units(1)
-        step(h_units(0), "svsv")
-        step(w1_units(0), "svsv")
+        step(h_units(0), "svsv", None, ())
+        step(w1_units(0), "svsv", None, ())
         spread_b1()
-        step(w1_units(1), "sssv", (0, A))
-        step(w1_units(2), "sssv", (1, A))
-        step(w1_units(3), "sssv", (2, A))
         repeat_vector(0)
+        repeat_vector(1)
+        repeat_vector(2)
+        step(w1_units(1), "svsv", (0, A), ())
+        step(w1_units(2), "sssv", (1, A), ())
+        step(w1_units(3), "sssv", (2, A), ())
         step(w2a[0:2], "sssv", (3, A), ())
         step(w2a[2:4], "sssv", None, ())
         step(w2b[0:2], "sssv", (0, B), (0,))
-        repeat_vector(1)
-        step(w2b[2:4], "ssss", (1, B), (1,))
-        repeat_vector(2)
+        step(w2b[2:4], "ssss", (1, B), ())
 
         products = {0: [(2, B), (3, B)], 1: [(0, C), (1, C)], 2: [(2, C), (3, C)], 3: [(0, E), (1, E)], 4: [(2, E), (3, E)]}
         unfinished = None
@@ -348,8 +349,10 @@ def tile_simplifiedretnet_pb_kernel(tc, h_ret, x, W1, b1, W2, b2, ln_g, ln_b, ou
             y, sums = add_residual(t, accs)
             for c2, tok in products.get(t, ()):
                 waiting.append(first_product(c2, tok))
-            if t + 1 not in (0, 1, S // P):
+            if t + 1 not in (0, 1, ) and t + 1 < S // P:
                 residual_tensor(t + 1)
+            if t in {0: 1}:
+                residual_vector({0: 1}[t])
             if t == 0:
                 todo.extend([(tile, unit[2], unit[3]) for unit, tile in zip(run, grouped)])
             if todo:

@@ -44,7 +44,7 @@ def tile_simplifiedretnet_pb_kernel(tc, h_ret, x, W1, b1, W2, b2, ln_g, ln_b, ou
         ident_bf16 = keep.tile([P, P], BF16)
         minus_half = keep.tile([P, 1], F32)
         nc.vector.memset(minus_half[:], -0.5)
-        ones = keep.tile([P, P], BF16)
+        ones = keep.tile([P, GROUP], BF16)
         nc.vector.memset(ones[:], 1.0)
 
         h_raw, w1_raw, w2_raw, x_raw = [], [], [], []
@@ -103,6 +103,11 @@ def tile_simplifiedretnet_pb_kernel(tc, h_ret, x, W1, b1, W2, b2, ln_g, ln_b, ou
         repeated = keep.tile([P, 3 * D], BF16)
         b2_all, gain_all, shift_all = [repeated[:, i * D : (i + 1) * D] for i in range(3)]
 
+        def warm_up():
+            bank = psum.tile([P, GROUP], F32, tag="bank")
+            for i in range(5):
+                nc.tensor.matmul(out=bank[:], lhsT=ones[:, :P], rhs=ones[:], start=True, stop=True)
+
         def spread_b1():
             bank = psum.tile([P, P], F32, tag="bank")
             nc.tensor.transpose(bank[:], b1_rows[:], ident[:])
@@ -112,7 +117,7 @@ def tile_simplifiedretnet_pb_kernel(tc, h_ret, x, W1, b1, W2, b2, ln_g, ln_b, ou
             bank = psum.tile([P, D], BF16, tag="bank")
             for half in range(D // GROUP):
                 cols = slice(i * D + half * GROUP, i * D + (half + 1) * GROUP)
-                nc.tensor.matmul(out=bank[:, group(half)], lhsT=ones[:], rhs=row0[:, cols], start=True, stop=True)
+                nc.tensor.matmul(out=bank[:, group(half)], lhsT=ones[:, :P], rhs=row0[:, cols], start=True, stop=True)
             nc.scalar.copy(out=repeated[:, i * D : (i + 1) * D], in_=bank[:])
 
         h_codes = keep.tile([P, H // K_PASS, S], U32, align_bytes=64)
@@ -228,7 +233,7 @@ def tile_simplifiedretnet_pb_kernel(tc, h_ret, x, W1, b1, W2, b2, ln_g, ln_b, ou
                     out=bank[:], lhsT=ident_bf16[:], rhs=x_raw[n][:, r * D + half * GROUP : r * D + (half + 1) * GROUP],
                     start=True, stop=False,
                 )
-                nc.tensor.matmul(out=bank[:], lhsT=ones[:], rhs=row0[:, cols], start=False, stop=True)
+                nc.tensor.matmul(out=bank[:], lhsT=ones[:, :P], rhs=row0[:, cols], start=False, stop=True)
                 nc.scalar.copy(out=xb[:, cols], in_=bank[:])
 
         def second_product(n, r):
@@ -324,6 +329,7 @@ def tile_simplifiedretnet_pb_kernel(tc, h_ret, x, W1, b1, W2, b2, ln_g, ln_b, ou
 
         A, B, C, E = tokens_of(0, 2), tokens_of(2, 2), tokens_of(4, 2), tokens_of(6, 2)
         w2a, w2b = w2_units(0), w2_units(1)
+        warm_up()
         step(h_units(0), "svsv", None, ())
         step(w1_units(0), "svsv", None, ())
         spread_b1()

@@ -16,6 +16,7 @@ PACK = 4
 K_PASS = P * PACK
 GROUP = 512
 TILES = GROUP // P
+PAIR = 2 * P
 
 S, H, F, D = 1024, 1024, 2048, 1024
 LN_EPS = 1e-5
@@ -37,7 +38,7 @@ def tile_simplifiedretnet_pb_kernel(tc, h_ret, x, W1, b1, W2, b2, ln_g, ln_b, ou
         x_groups = x.flatten_outer_dims().rearrange(tokens, m=P, r=TILES)
         out_groups = out.flatten_outer_dims().rearrange("(n m r) d -> n m r d", m=P, r=TILES)
         w1_groups = W1.rearrange("(c u m e) k -> c u m (e k)", u=2, m=P, e=2)
-        w2_pairs = W2.rearrange("(n r m) k -> n m r k", r=2, m=P)
+        w2_parts = W2.rearrange("(n r m) (c k) -> n c m r k", r=TILES, m=P, c=2)
 
         ident = keep.tile([P, P], F32)
         make_identity(nc, ident[:])
@@ -49,16 +50,16 @@ def tile_simplifiedretnet_pb_kernel(tc, h_ret, x, W1, b1, W2, b2, ln_g, ln_b, ou
 
         h_raw, w1_raw, w2_raw, x_raw = [], [], [], []
 
-        def load_h(n):
-            rows = raw.tile([P, TILES * H], BF16, tag="h", bufs=2)
-            for half in range(2):
-                cols = slice(half * 2 * H, (half + 1) * 2 * H)
-                nc.sync.dma_start(out=rows[:, cols], in_=h_groups[n][:, cols])
+        def load_h(g):
+            rows = raw.tile([P, 2 * H], BF16, tag="h")
+            n, half = divmod(g, 2)
+            nc.sync.dma_start(out=rows[:], in_=h_groups[n][:, half * 2 * H : (half + 1) * 2 * H])
             h_raw.append(rows)
 
-        def load_x(n):
-            rows = raw.tile([P, TILES * D], BF16, tag="x", bufs=2)
-            nc.sync.dma_start(out=rows[:], in_=x_groups[n])
+        def load_x(g):
+            rows = raw.tile([P, 2 * D], BF16, tag="x")
+            n, half = divmod(g, 2)
+            nc.sync.dma_start(out=rows[:], in_=x_groups[n][:, half * 2 * D : (half + 1) * 2 * D])
             x_raw.append(rows)
 
         def load_w1(c):
@@ -67,9 +68,9 @@ def tile_simplifiedretnet_pb_kernel(tc, h_ret, x, W1, b1, W2, b2, ln_g, ln_b, ou
                 nc.sync.dma_start(out=rows[:, u * 2 * H : (u + 1) * 2 * H], in_=w1_groups[c, u])
             w1_raw.append(rows)
 
-        def load_w2(n):
-            rows = raw.tile([P, 2 * F], BF16, tag="w2")
-            nc.sync.dma_start(out=rows[:].rearrange("m (r k) -> m r k", r=2), in_=w2_pairs[n])
+        def load_w2(n, part):
+            rows = raw.tile([P, TILES * F // 2], BF16, tag="w2")
+            nc.sync.dma_start(out=rows[:].rearrange("m (r k) -> m r k", r=TILES), in_=w2_parts[n, part])
             w2_raw.append(rows)
 
         b1_rows = keep.tile([P, P], F32)
@@ -87,11 +88,17 @@ def tile_simplifiedretnet_pb_kernel(tc, h_ret, x, W1, b1, W2, b2, ln_g, ln_b, ou
         nc.scalar.activation(out=warm[:], in_=minus_half[:], func=ACT.Gelu)
         for c in range(1, F // GROUP):
             load_w1(c)
-        for n in range(D // (2 * P)):
-            load_w2(n)
-        load_x(0)
         load_h(1)
+        load_w2(0, 0)
+        load_w2(0, 1)
+        load_w2(1, 0)
+        load_w2(1, 1)
+        load_x(0)
+        load_h(2)
         load_x(1)
+        load_h(3)
+        load_x(2)
+        load_x(3)
 
         nc.vector.tensor_copy(out=ident_bf16[:], in_=ident[:])
 
@@ -120,8 +127,8 @@ def tile_simplifiedretnet_pb_kernel(tc, h_ret, x, W1, b1, W2, b2, ln_g, ln_b, ou
                 nc.tensor.matmul(out=bank[:, group(half)], lhsT=ones[:, :P], rhs=row0[:, cols], start=True, stop=True)
             nc.scalar.copy(out=repeated[:, i * D : (i + 1) * D], in_=bank[:])
 
-        h_codes = keep.tile([P, H // K_PASS, S], U32, align_bytes=64)
-        h_scales = keep.tile([P, H // K_PASS, S], U8, align_bytes=64)
+        h_codes = keep.tile([P, S // PAIR, H // K_PASS, PAIR], U32, align_bytes=64)
+        h_scales = keep.tile([P, S // PAIR, H // K_PASS, PAIR], U8, align_bytes=64)
         w1_codes = keep.tile([P, H // K_PASS, F], U32, align_bytes=64)
         w1_scales = keep.tile([P, H // K_PASS, F], U8, align_bytes=64)
         w2_codes = keep.tile([P, F // K_PASS, D], U32, align_bytes=64)
@@ -133,33 +140,41 @@ def tile_simplifiedretnet_pb_kernel(tc, h_ret, x, W1, b1, W2, b2, ln_g, ln_b, ou
             words = rows[:].bitcast(F32).rearrange("m (r w) -> m r w", r=n)
             return [words[:, r, :] for r in range(n)]
 
-        def units_of(row_tiles, codes, scales, cols):
-            return [(row_tiles, c, codes[:, c, cols], scales[:, c, cols]) for c in range(codes.shape[1])]
-
-        def h_units(n):
-            return units_of(word_tiles(h_raw[n], TILES), h_codes, h_scales, group(n))
+        def h_unit(g):
+            row_tiles = word_tiles(h_raw[g], 2)
+            banks = [(row_tiles, c) for c in range(H // K_PASS)]
+            flat = "p c m -> p (c m)"
+            return banks, h_codes[:, g, :, :].rearrange(flat), h_scales[:, g, :, :].rearrange(flat)
 
         def w1_units(c2):
-            return units_of(word_tiles(w1_raw[c2], TILES), w1_codes, w1_scales, group(c2))
+            tiles = word_tiles(w1_raw[c2], TILES)
+            return [
+                ([(tiles[0:2], c), (tiles[2:4], c)], w1_codes[:, c, group(c2)], w1_scales[:, c, group(c2)])
+                for c in range(H // K_PASS)
+            ]
 
         def w2_units(half):
-            row_tiles = word_tiles(w2_raw[2 * half], 2) + word_tiles(w2_raw[2 * half + 1], 2)
-            return units_of(row_tiles, w2_codes, w2_scales, group(half))
+            units = []
+            for part in range(2):
+                tiles = word_tiles(w2_raw[2 * half + part], TILES)
+                for i in range(2):
+                    c = 2 * part + i
+                    banks = [(tiles[0:2], i), (tiles[2:4], i)]
+                    units.append((banks, w2_codes[:, c, group(half)], w2_scales[:, c, group(half)]))
+            return units
 
         def transpose_run(run, engines):
             grouped = [stage.tile([P, GROUP * PACK], BF16, align_bytes=64, tag="grouped", bufs=5, name="grouped") for unit in run]
             which = 0
             for half in range(2):
                 for unit, dst_tile in zip(run, grouped):
-                    row_tiles, c = unit[0], unit[1]
+                    row_tiles, c = unit[0][half]
                     bank = psum.tile([P, 2, 2 * P], F32, tag="bank")
                     for r in range(2):
                         for u in range(2):
                             first = (2 * c + u) * P
                             nc.tensor.transpose(
-                                bank[:, u, r * P : (r + 1) * P],
-                                row_tiles[2 * half + r][:, first : first + P],
-                                ident[:],
+                                bank[:, u, r * P : (r + 1) * P], row_tiles[r][:, first : first + P], ident[:]
                             )
                     words = dst_tile[:].bitcast(F32).rearrange("p (r u) -> p r u", u=2)
                     dst = words[:, half * 2 * P : (half + 1) * 2 * P, :]
@@ -174,8 +189,8 @@ def tile_simplifiedretnet_pb_kernel(tc, h_ret, x, W1, b1, W2, b2, ln_g, ln_b, ou
         def quantise(grouped, codes, scales):
             nc.vector.quantize_mx(out=codes.bitcast(FP8X4), scales=scales, in_=grouped[:])
 
-        def first_product(c2, tok):
-            width = tok.stop - tok.start
+        def first_product(c2, g):
+            width = PAIR
             g_plain = stage.tile([P, PACK, width], BF16, tag="g_plain", bufs=3)
             share = GROUP // width
             for first in range(0, PACK, share):
@@ -188,8 +203,8 @@ def tile_simplifiedretnet_pb_kernel(tc, h_ret, x, W1, b1, W2, b2, ln_g, ln_b, ou
                             out=bank[:, i, :],
                             lhsT=w1_codes[:, c, rows].bitcast(FP8X4),
                             lhsT_scale=w1_scales[:, c, rows],
-                            rhs=h_codes[:, c, tok].bitcast(FP8X4),
-                            rhs_scale=h_scales[:, c, tok],
+                            rhs=h_codes[:, g, c, :].bitcast(FP8X4),
+                            rhs_scale=h_scales[:, g, c, :],
                             start=(c == 0),
                             stop=(c == H // K_PASS - 1),
                         )
@@ -198,7 +213,7 @@ def tile_simplifiedretnet_pb_kernel(tc, h_ret, x, W1, b1, W2, b2, ln_g, ln_b, ou
                     nc.scalar.activation(
                         out=g_plain[:, first + i, :], in_=bank[:, i, :], func=ACT.Gelu, bias=b1_cols[:, j : j + 1], scale=1.0
                     )
-            return g_plain, c2, tok
+            return g_plain, c2, slice(g * PAIR, (g + 1) * PAIR)
 
         def regroup(g_plain):
             grouped = stage.tile([P, g_plain.shape[1] * g_plain.shape[2]], BF16, align_bytes=64, tag="grouped", bufs=5)
@@ -218,19 +233,19 @@ def tile_simplifiedretnet_pb_kernel(tc, h_ret, x, W1, b1, W2, b2, ln_g, ln_b, ou
             return xb_tiles[tile_index]
 
         def residual_vector(tile_index):
-            n, r = divmod(tile_index, TILES)
+            g, r = divmod(tile_index, 2)
             nc.vector.tensor_tensor(
-                out=xb_tile(tile_index), in0=x_raw[n][:, r * D : (r + 1) * D], in1=b2_all, op=ALU.add
+                out=xb_tile(tile_index), in0=x_raw[g][:, r * D : (r + 1) * D], in1=b2_all, op=ALU.add
             )
 
         def residual_tensor(tile_index):
-            n, r = divmod(tile_index, TILES)
+            g, r = divmod(tile_index, 2)
             xb = xb_tile(tile_index)
             for half in range(D // GROUP):
                 cols = slice(half * GROUP, (half + 1) * GROUP)
                 bank = psum.tile([P, GROUP], F32, tag="bank")
                 nc.tensor.matmul(
-                    out=bank[:], lhsT=ident_bf16[:], rhs=x_raw[n][:, r * D + half * GROUP : r * D + (half + 1) * GROUP],
+                    out=bank[:], lhsT=ident_bf16[:], rhs=x_raw[g][:, r * D + half * GROUP : r * D + (half + 1) * GROUP],
                     start=True, stop=False,
                 )
                 nc.tensor.matmul(out=bank[:], lhsT=ones[:, :P], rhs=row0[:, cols], start=False, stop=True)
@@ -312,11 +327,11 @@ def tile_simplifiedretnet_pb_kernel(tc, h_ret, x, W1, b1, W2, b2, ln_g, ln_b, ou
             return todo
 
         def step(run=(), engines="", product=None, extra=()):
-            grouped = transpose_run(run, engines) if run else []
+            grouped = transpose_run(run, engines)
             new = first_product(*product) if product else None
             todo = start_grouping()
             for unit, tile in zip(run, grouped):
-                todo.insert(0, (tile, unit[2], unit[3]))
+                todo.insert(0, (tile, unit[1], unit[2]))
             for t in extra:
                 residual_vector(t)
             for item in todo:
@@ -324,43 +339,39 @@ def tile_simplifiedretnet_pb_kernel(tc, h_ret, x, W1, b1, W2, b2, ln_g, ln_b, ou
             if product:
                 waiting.append(new)
 
-        def tokens_of(first, count):
-            return slice(first * P, (first + count) * P)
-
-        A, B, C, E = tokens_of(0, 2), tokens_of(2, 2), tokens_of(4, 2), tokens_of(6, 2)
         w2a, w2b = w2_units(0), w2_units(1)
         warm_up()
-        step(h_units(0), "svsv", None, ())
-        step(w1_units(0), "svsv", None, ())
+        step([h_unit(0)], "sv", None, ())
+        step([*w1_units(0)], "svsv", None, ())
         spread_b1()
         repeat_vector(0)
         repeat_vector(1)
         repeat_vector(2)
-        step(w1_units(1), "svsv", (0, A), ())
-        step(w1_units(2), "sssv", (1, A), ())
-        step(w1_units(3), "sssv", (2, A), ())
-        step(w2a[0:2], "sssv", (3, A), ())
-        step(w2a[2:4], "sssv", None, ())
-        step(w2b[0:2], "sssv", (0, B), (0,))
-        step(w2b[2:4], "ssss", (1, B), ())
+        step([*w1_units(1)], "svsv", (0, 0), ())
+        step([*w1_units(2)], "svsv", (1, 0), ())
+        step([*w1_units(3)], "sssv", (2, 0), ())
+        step([h_unit(1)], "sv", None, ())
+        step([*w2a[0:2]], "sssv", (3, 0), ())
+        step([*w2a[2:4]], "sssv", None, ())
+        step([*w2b[0:2]], "sssv", (0, 1), ())
+        step([*w2b[2:4]], "ssss", (1, 1), (0,))
 
-        products = {0: [(2, B), (3, B)], 1: [(0, C), (1, C)], 2: [(2, C), (3, C)], 3: [(0, E), (1, E)], 4: [(2, E), (3, E)]}
+        products = {0: [(2, 1), (3, 1)], 1: [(0, 2), (1, 2)], 2: [(2, 2), (3, 2)], 3: [(0, 3), (1, 3)], 4: [(2, 3), (3, 3)]}
+        runs = {0: [h_unit(2)], 2: [h_unit(3)]}
         unfinished = None
         for t in range(S // P):
             accs = second_product(t // TILES, t % TILES)
-            if t == 0:
-                run = h_units(1)
-                grouped = transpose_run(run, "ssss")
+            run = runs.get(t, ())
+            grouped = transpose_run(run, "ssss")
             todo = start_grouping()
             y, sums = add_residual(t, accs)
-            for c2, tok in products.get(t, ()):
-                waiting.append(first_product(c2, tok))
-            if t + 1 not in (0, 1, ) and t + 1 < S // P:
-                residual_tensor(t + 1)
-            if t in {0: 1}:
-                residual_vector({0: 1}[t])
+            for c2, g in products.get(t, ()):
+                waiting.append(first_product(c2, g))
             if t == 0:
-                todo.extend([(tile, unit[2], unit[3]) for unit, tile in zip(run, grouped)])
+                residual_vector(1)
+            elif t + 1 < S // P:
+                residual_tensor(t + 1)
+            todo.extend([(tile, unit[1], unit[2]) for unit, tile in zip(run, grouped)])
             if todo:
                 quantise(*todo.pop(0))
             neg_mean = negative_mean(sums)

@@ -70,7 +70,11 @@ def tile_simplifiedretnet_pb_kernel(tc, h_ret, x, W1, b1, W2, b2, ln_g, ln_b, ou
 
         def load_w2(n, part):
             rows = raw.tile([P, TILES * F // 2], BF16, tag="w2")
-            nc.sync.dma_start(out=rows[:].rearrange("m (r k) -> m r k", r=TILES), in_=w2_parts[n, part])
+            for half in range(2):
+                nc.sync.dma_start(
+                    out=rows[:, half * F : (half + 1) * F].rearrange("m (r k) -> m r k", r=2),
+                    in_=w2_parts[n, part, :, 2 * half : 2 * half + 2, :],
+                )
             w2_raw.append(rows)
 
         b1_rows = keep.tile([P, P], F32)
@@ -352,11 +356,11 @@ def tile_simplifiedretnet_pb_kernel(tc, h_ret, x, W1, b1, W2, b2, ln_g, ln_b, ou
         step([*w1_units(3)], "sssv", (2, 0), ())
         step([h_unit(1)], "sv", None, ())
         step([*w2a[0:2]], "sssv", (3, 0), ())
-        step([*w2a[2:4]], "sssv", None, ())
-        step([*w2b[0:2]], "sssv", (0, 1), ())
-        step([*w2b[2:4]], "ssss", (1, 1), (0,))
+        step([*w2a[2:4]], "sssv", (0, 1), ())
+        step([*w2b[0:2]], "sssv", (1, 1), ())
+        step([*w2b[2:4]], "ssss", (2, 1), (0,))
 
-        products = {0: [(2, 1), (3, 1)], 1: [(0, 2), (1, 2)], 2: [(2, 2), (3, 2)], 3: [(0, 3), (1, 3)], 4: [(2, 3), (3, 3)]}
+        products = {0: [(3, 1)], 1: [(0, 2), (1, 2)], 2: [(2, 2), (3, 2)], 3: [(0, 3), (1, 3)], 4: [(2, 3), (3, 3)]}
         runs = {0: [h_unit(2)], 2: [h_unit(3)]}
         unfinished = None
         for t in range(S // P):

from contextlib import ExitStack

import concourse.mybir as mybir
from concourse.masks import make_identity

F32 = mybir.dt.float32
BF16 = mybir.dt.bfloat16
U32 = mybir.dt.uint32
U8 = mybir.dt.uint8
FP8X4 = mybir.dt.float8_e4m3fn_x4
ALU = mybir.AluOpType
ACT = mybir.ActivationFunctionType

P = 128
PACK = 4
K_PASS = P * PACK
GROUP = 512
TILES = GROUP // P
PAIR = 2 * P

S, H, F, D = 1024, 1024, 2048, 1024
LN_EPS = 1e-5
FLOPS = 2 * S * H * F + 2 * S * F * D


def tile_simplifiedretnet_pb_kernel(tc, h_ret, x, W1, b1, W2, b2, ln_g, ln_b, out):
    nc = tc.nc
    with ExitStack() as ctx:
        keep = ctx.enter_context(tc.tile_pool(name="keep", bufs=1))
        raw = ctx.enter_context(tc.tile_pool(name="raw", bufs=4))
        stage = ctx.enter_context(tc.tile_pool(name="stage", bufs=2))
        stats = ctx.enter_context(tc.tile_pool(name="stats", bufs=4))
        psum = ctx.enter_context(tc.psum_pool(name="psum", bufs=8))
        ctx.enter_context(tc.manual_schedule())

        tokens = "(n m r) k -> n m (r k)"
        h_groups = h_ret.flatten_outer_dims().rearrange(tokens, m=P, r=TILES)
        x_groups = x.flatten_outer_dims().rearrange(tokens, m=P, r=TILES)
        out_groups = out.flatten_outer_dims().rearrange("(n m r) d -> n m r d", m=P, r=TILES)
        w1_groups = W1.rearrange("(c u m e) k -> c u m (e k)", u=2, m=P, e=2)
        w2_parts = W2.rearrange("(n r m) (c k) -> n c m r k", r=TILES, m=P, c=2)

        ident = keep.tile([P, P], F32)
        make_identity(nc, ident[:])
        ident_bf16 = keep.tile([P, P], BF16)
        minus_half = keep.tile([P, 1], F32)
        nc.vector.memset(minus_half[:], -0.5)
        ones = keep.tile([P, GROUP], BF16)
        nc.vector.memset(ones[:], 1.0)

        h_raw, w1_raw, w2_raw, x_raw = [], [], [], []

        def load_h(g):
            rows = raw.tile([P, 2 * H], BF16, tag="h")
            n, half = divmod(g, 2)
            nc.sync.dma_start(out=rows[:], in_=h_groups[n][:, half * 2 * H : (half + 1) * 2 * H])
            h_raw.append(rows)

        def load_x(g):
            rows = raw.tile([P, 2 * D], BF16, tag="x")
            n, half = divmod(g, 2)
            nc.sync.dma_start(out=rows[:], in_=x_groups[n][:, half * 2 * D : (half + 1) * 2 * D])
            x_raw.append(rows)

        def load_w1(c):
            rows = raw.tile([P, TILES * H], BF16, tag="w1_then_xb")
            for u in range(2):
                nc.sync.dma_start(out=rows[:, u * 2 * H : (u + 1) * 2 * H], in_=w1_groups[c, u])
            w1_raw.append(rows)

        def load_w2(n, part):
            rows = raw.tile([P, TILES * F // 2], BF16, tag="w2")
            for half in range(2):
                nc.sync.dma_start(
                    out=rows[:, half * F : (half + 1) * F].rearrange("m (r k) -> m r k", r=2),
                    in_=w2_parts[n, part, :, 2 * half : 2 * half + 2, :],
                )
            w2_raw.append(rows)

        b1_rows = keep.tile([P, P], F32)
        nc.vector.memset(b1_rows[:], 0.0)
        row0 = keep.tile([P, 3 * D], BF16)
        nc.vector.memset(row0[:].bitcast(F32), 0.0)
        load_h(0)
        load_w1(0)
        nc.scalar.dma_start(
            out=b1_rows[0 : F // (2 * P), :].bitcast(BF16), in_=b1.rearrange("(a w) -> a w", w=2 * P)
        )
        for i, vector in enumerate((b2, ln_g, ln_b)):
            nc.scalar.dma_start(out=row0[0:1, i * D : (i + 1) * D], in_=vector.unsqueeze(0))
        warm = keep.tile([P, 1], F32)
        nc.scalar.activation(out=warm[:], in_=minus_half[:], func=ACT.Gelu)
        for c in range(1, F // GROUP):
            load_w1(c)
        load_h(1)
        load_w2(0, 0)
        load_w2(0, 1)
        load_w2(1, 0)
        load_w2(1, 1)
        load_x(0)
        load_h(2)
        load_x(1)
        load_h(3)
        load_x(2)
        load_x(3)

        nc.vector.tensor_copy(out=ident_bf16[:], in_=ident[:])

        def group(n):
            return slice(n * GROUP, (n + 1) * GROUP)

        b1_words = keep.tile([P, F // (2 * P)], F32)
        b1_cols = b1_words[:].bitcast(BF16)
        repeated = keep.tile([P, 3 * D], BF16)
        b2_all, gain_all, shift_all = [repeated[:, i * D : (i + 1) * D] for i in range(3)]

        def warm_up():
            bank = psum.tile([P, GROUP], F32, tag="bank")
            for i in range(5):
                nc.tensor.matmul(out=bank[:], lhsT=ones[:, :P], rhs=ones[:], start=True, stop=True)

        def spread_b1():
            bank = psum.tile([P, P], F32, tag="bank")
            nc.tensor.transpose(bank[:], b1_rows[:], ident[:])
            nc.scalar.copy(out=b1_words[:], in_=bank[:, : F // (2 * P)])

        def repeat_vector(i):
            bank = psum.tile([P, D], BF16, tag="bank")
            for half in range(D // GROUP):
                cols = slice(i * D + half * GROUP, i * D + (half + 1) * GROUP)
                nc.tensor.matmul(out=bank[:, group(half)], lhsT=ones[:, :P], rhs=row0[:, cols], start=True, stop=True)
            nc.scalar.copy(out=repeated[:, i * D : (i + 1) * D], in_=bank[:])

        h_codes = keep.tile([P, S // PAIR, H // K_PASS, PAIR], U32, align_bytes=64)
        h_scales = keep.tile([P, S // PAIR, H // K_PASS, PAIR], U8, align_bytes=64)
        w1_codes = keep.tile([P, H // K_PASS, F], U32, align_bytes=64)
        w1_scales = keep.tile([P, H // K_PASS, F], U8, align_bytes=64)
        w2_codes = keep.tile([P, F // K_PASS, D], U32, align_bytes=64)
        w2_scales = keep.tile([P, F // K_PASS, D], U8, align_bytes=64)
        g_codes = keep.tile([P, F // K_PASS, S], U32, align_bytes=64)
        g_scales = keep.tile([P, F // K_PASS, S], U8, align_bytes=64)

        def word_tiles(rows, n):
            words = rows[:].bitcast(F32).rearrange("m (r w) -> m r w", r=n)
            return [words[:, r, :] for r in range(n)]

        def h_unit(g):
            row_tiles = word_tiles(h_raw[g], 2)
            banks = [(row_tiles, c) for c in range(H // K_PASS)]
            flat = "p c m -> p (c m)"
            return banks, h_codes[:, g, :, :].rearrange(flat), h_scales[:, g, :, :].rearrange(flat)

        def w1_units(c2):
            tiles = word_tiles(w1_raw[c2], TILES)
            return [
                ([(tiles[0:2], c), (tiles[2:4], c)], w1_codes[:, c, group(c2)], w1_scales[:, c, group(c2)])
                for c in range(H // K_PASS)
            ]

        def w2_units(half):
            units = []
            for part in range(2):
                tiles = word_tiles(w2_raw[2 * half + part], TILES)
                for i in range(2):
                    c = 2 * part + i
                    banks = [(tiles[0:2], i), (tiles[2:4], i)]
                    units.append((banks, w2_codes[:, c, group(half)], w2_scales[:, c, group(half)]))
            return units

        def transpose_run(run, engines):
            grouped = [stage.tile([P, GROUP * PACK], BF16, align_bytes=64, tag="grouped", bufs=5, name="grouped") for unit in run]
            which = 0
            for half in range(2):
                for unit, dst_tile in zip(run, grouped):
                    row_tiles, c = unit[0][half]
                    bank = psum.tile([P, 2, 2 * P], F32, tag="bank")
                    for r in range(2):
                        for u in range(2):
                            first = (2 * c + u) * P
                            nc.tensor.transpose(
                                bank[:, u, r * P : (r + 1) * P], row_tiles[r][:, first : first + P], ident[:]
                            )
                    words = dst_tile[:].bitcast(F32).rearrange("p (r u) -> p r u", u=2)
                    dst = words[:, half * 2 * P : (half + 1) * 2 * P, :]
                    src = bank[:].rearrange("p u r -> p r u")
                    if engines[which] == "v":
                        nc.vector.tensor_copy(out=dst, in_=src)
                    else:
                        nc.scalar.copy(out=dst, in_=src)
                    which += 1
            return grouped

        def quantise(grouped, codes, scales):
            nc.vector.quantize_mx(out=codes.bitcast(FP8X4), scales=scales, in_=grouped[:])

        def first_product(c2, g):
            width = PAIR
            g_plain = stage.tile([P, PACK, width], BF16, tag="g_plain", bufs=3)
            share = GROUP // width
            for first in range(0, PACK, share):
                bank = psum.tile([P, share, width], F32, tag="bank")
                for i in range(share):
                    t = first + i
                    rows = slice(c2 * GROUP + t * P, c2 * GROUP + (t + 1) * P)
                    for c in range(H // K_PASS):
                        nc.tensor.matmul_mx(
                            out=bank[:, i, :],
                            lhsT=w1_codes[:, c, rows].bitcast(FP8X4),
                            lhsT_scale=w1_scales[:, c, rows],
                            rhs=h_codes[:, g, c, :].bitcast(FP8X4),
                            rhs_scale=h_scales[:, g, c, :],
                            start=(c == 0),
                            stop=(c == H // K_PASS - 1),
                        )
                for i in range(share):
                    j = c2 * PACK + first + i
                    nc.scalar.activation(
                        out=g_plain[:, first + i, :], in_=bank[:, i, :], func=ACT.Gelu, bias=b1_cols[:, j : j + 1], scale=1.0
                    )
            return g_plain, c2, slice(g * PAIR, (g + 1) * PAIR)

        def regroup(g_plain):
            grouped = stage.tile([P, g_plain.shape[1] * g_plain.shape[2]], BF16, align_bytes=64, tag="grouped", bufs=5)
            nc.vector.tensor_copy(
                out=grouped[:].rearrange("p (a i t) -> p a t i", i=4, t=PACK),
                in_=g_plain[:].rearrange("p t (a i) -> p a t i", i=4),
            )
            return grouped

        xb_tiles = [None] * (S // P)

        def xb_tile(tile_index):
            if xb_tiles[tile_index] is None:
                xb = raw.tile([P, 2, D], F32, tag="w1_then_xb")
                xb_tiles[tile_index] = xb[:, 0, :]
                xb_tiles[tile_index + 1] = xb[:, 1, :]
            return xb_tiles[tile_index]

        def residual_vector(tile_index):
            g, r = divmod(tile_index, 2)
            nc.vector.tensor_tensor(
                out=xb_tile(tile_index), in0=x_raw[g][:, r * D : (r + 1) * D], in1=b2_all, op=ALU.add
            )

        def residual_tensor(tile_index):
            g, r = divmod(tile_index, 2)
            xb = xb_tile(tile_index)
            for half in range(D // GROUP):
                cols = slice(half * GROUP, (half + 1) * GROUP)
                bank = psum.tile([P, GROUP], F32, tag="bank")
                nc.tensor.matmul(
                    out=bank[:], lhsT=ident_bf16[:], rhs=x_raw[g][:, r * D + half * GROUP : r * D + (half + 1) * GROUP],
                    start=True, stop=False,
                )
                nc.tensor.matmul(out=bank[:], lhsT=ones[:, :P], rhs=row0[:, cols], start=False, stop=True)
                nc.scalar.copy(out=xb[:, cols], in_=bank[:])

        def second_product(n, r):
            tok = slice(n * GROUP + r * P, n * GROUP + (r + 1) * P)
            accs = []
            for half in range(D // GROUP):
                acc = psum.tile([P, GROUP], F32, tag="bank")
                for c in range(F // K_PASS):
                    nc.tensor.matmul_mx(
                        out=acc[:],
                        lhsT=g_codes[:, c, tok].bitcast(FP8X4),
                        lhsT_scale=g_scales[:, c, tok],
                        rhs=w2_codes[:, c, group(half)].bitcast(FP8X4),
                        rhs_scale=w2_scales[:, c, group(half)],
                        start=(c == 0),
                        stop=(c == F // K_PASS - 1),
                    )
                accs.append(acc)
            return accs

        def add_residual(tile_index, accs):
            y = stage.tile([P, D], F32, tag="y", bufs=2)
            sums = stats.tile([P, 2], F32, tag="sums")
            for half in range(D // GROUP):
                nc.vector.scalar_tensor_tensor(
                    out=y[:, group(half)],
                    in0=accs[half][:],
                    scalar=1.0,
                    in1=xb_tiles[tile_index][:, group(half)],
                    op0=ALU.mult,
                    op1=ALU.add,
                    accum_out=sums[:, half : half + 1],
                )
            return y, sums

        def negative_mean(sums):
            neg_mean = stats.tile([P, 1], F32, tag="neg_mean")
            nc.vector.tensor_scalar(
                out=neg_mean[:], in0=sums[:, 0:1], scalar1=sums[:, 1:2], scalar2=-1.0 / D, op0=ALU.add, op1=ALU.mult
            )
            return neg_mean

        def inverse_deviation(y, neg_mean):
            squares = stage.tile([P, D], BF16, tag="squares", bufs=1)
            var = stats.tile([P, 1], F32, tag="var")
            nc.scalar.activation(
                out=squares[:], in_=y[:], func=ACT.Square, bias=neg_mean[:], scale=1.0, accum_out=var[:]
            )
            rstd = stats.tile([P, 2], F32, tag="rstd")
            nc.gpsimd.tensor_scalar(
                out=rstd[:, 0:1], in0=var[:], scalar1=1.0 / D, scalar2=LN_EPS, op0=ALU.mult, op1=ALU.add
            )
            nc.gpsimd.tensor_tensor(out=rstd[:, 1:2], in0=rstd[:, 0:1], in1=minus_half[:], op=ALU.pow)
            return rstd[:, 1:2]

        def centre_and_gain(y, neg_mean):
            normed = stage.tile([P, D], F32, tag="normed", bufs=3)
            nc.vector.scalar_tensor_tensor(
                out=normed[:], in0=y[:], scalar=neg_mean[:], in1=gain_all, op0=ALU.add, op1=ALU.mult
            )
            return normed

        def scale_shift_store(tile_index, normed, rstd, half):
            n, r = divmod(tile_index, TILES)
            cols = group(half)
            nc.vector.scalar_tensor_tensor(
                out=normed[:, cols], in0=normed[:, cols], scalar=rstd, in1=shift_all[:, cols], op0=ALU.mult, op1=ALU.add
            )
            nc.sync.dma_start(out=out_groups[n][:, r, cols], in_=normed[:, cols])

        waiting = []

        def start_grouping():
            todo = [(regroup(g), g_codes[:, c2, tok], g_scales[:, c2, tok]) for g, c2, tok in waiting]
            waiting.clear()
            return todo

        def step(run=(), engines="", product=None, extra=()):
            grouped = transpose_run(run, engines)
            new = first_product(*product) if product else None
            todo = start_grouping()
            for unit, tile in zip(run, grouped):
                todo.insert(0, (tile, unit[1], unit[2]))
            for t in extra:
                residual_vector(t)
            for item in todo:
                quantise(*item)
            if product:
                waiting.append(new)

        w2a, w2b = w2_units(0), w2_units(1)
        warm_up()
        step([h_unit(0)], "sv", None, ())
        step([*w1_units(0)], "svsv", None, ())
        spread_b1()
        repeat_vector(0)
        repeat_vector(1)
        repeat_vector(2)
        step([*w1_units(1)], "svsv", (0, 0), ())
        step([*w1_units(2)], "svsv", (1, 0), ())
        step([*w1_units(3)], "sssv", (2, 0), ())
        step([h_unit(1)], "sv", None, ())
        step([*w2a[0:2]], "sssv", (3, 0), ())
        step([*w2a[2:4]], "sssv", (0, 1), ())
        step([*w2b[0:2]], "sssv", (1, 1), ())
        step([*w2b[2:4]], "ssss", (2, 1), (0,))

        products = {0: [(3, 1)], 1: [(0, 2), (1, 2)], 2: [(2, 2), (3, 2)], 3: [(0, 3), (1, 3)], 4: [(2, 3), (3, 3)]}
        runs = {0: [h_unit(2)], 2: [h_unit(3)]}
        unfinished = None
        for t in range(S // P):
            accs = second_product(t // TILES, t % TILES)
            run = runs.get(t, ())
            grouped = transpose_run(run, "ssss")
            todo = start_grouping()
            y, sums = add_residual(t, accs)
            for c2, g in products.get(t, ()):
                waiting.append(first_product(c2, g))
            if t == 0:
                residual_vector(1)
            elif t + 1 < S // P:
                residual_tensor(t + 1)
            todo.extend([(tile, unit[1], unit[2]) for unit, tile in zip(run, grouped)])
            if todo:
                quantise(*todo.pop(0))
            neg_mean = negative_mean(sums)
            rstd = inverse_deviation(y, neg_mean)
            while todo:
                quantise(*todo.pop(0))
            if unfinished is not None:
                scale_shift_store(*unfinished, 0)
                scale_shift_store(*unfinished, 1)
            normed = centre_and_gain(y, neg_mean)
            unfinished = (t, normed, rstd)
        scale_shift_store(*unfinished, 0)
        scale_shift_store(*unfinished, 1)
